import numpy as np
import ml_dtypes


def mxq(x, axis, fmt="e4m3"):
    dtype, down = {"e4m3": (ml_dtypes.float8_e4m3fn, 7), "e5m2": (ml_dtypes.float8_e5m2, 14)}[fmt]
    v = np.moveaxis(np.asarray(x, np.float32).astype(ml_dtypes.bfloat16).astype(np.float64), axis, -1)
    blocks = v.reshape(v.shape[:-1] + (-1, 32))
    amax = np.abs(blocks).max(-1, keepdims=True)
    byte = np.maximum(np.where(amax > 0, np.frexp(amax)[1] - 1 + 127, 0) - down, 1)
    scale = np.exp2(byte - 127.0)
    codes = (blocks / scale).astype(np.float32).astype(dtype).astype(np.float64)
    return np.moveaxis((codes * scale).reshape(v.shape), -1, axis)


WIDE = False


def mx_kscale(k):
    if not WIDE:
        return np.ones(k)
    levels = np.array([10, -10, 5, -5, 0])
    a = np.random.permutation(np.resize(levels, k // 512 * 4)).reshape(k // 512, 4)
    idx = np.arange(k)
    return np.exp2(a[idx // 512, idx % 128 // 32])


BF16 = ml_dtypes.bfloat16


def bf(x):
    return np.asarray(x, np.float32).astype(BF16)


def f64(x):
    return np.asarray(x).astype(np.float64)


E2M1 = np.array([0.0, 0.5, 1.0, 1.5, 2.0, 3.0, 4.0, 6.0, -0.0, -0.5, -1.0, -1.5, -2.0, -3.0, -4.0, -6.0])


def pack_weight(w, fmt):
    k, n = w.shape
    w = f64(bf(w)).reshape(k // 32, 32, n)
    amax = np.abs(w).max(1)
    if fmt == "e4m3":
        byte = np.frexp(amax)[1] - 1 + 127 - 7
    else:
        mant, ex = np.frexp(amax / 6.0)
        byte = np.where(mant > 0.5, ex, ex - 1) + 127
    byte = np.clip(np.where(amax > 0, byte, 1), 1, 254)
    scaled = (w * np.exp2(127.0 - byte)[:, None, :]).reshape(k, n).astype(np.float32)
    by_word = np.ascontiguousarray(scaled.reshape(k // 512, 128, 4, n).transpose(0, 1, 3, 2))
    if fmt == "e4m3":
        words = by_word.astype(ml_dtypes.float8_e4m3fn).view(np.uint8)
    else:
        c = by_word.astype(ml_dtypes.float4_e2m1fn).view(np.uint8) & 0xF
        words = c[..., 0::2] | (c[..., 1::2] << 4)
    return np.ascontiguousarray(words), np.ascontiguousarray(byte.astype(np.uint8).reshape(k // 512, 16, n))


def unpack_weight(words, scales, fmt):
    g, p, n, _ = words.shape
    if fmt == "e4m3":
        vals = np.ascontiguousarray(words).view(ml_dtypes.float8_e4m3fn).astype(np.float64)
    else:
        nib = np.empty((g, p, n, 4), np.uint8)
        nib[..., 0::2] = words & 0xF
        nib[..., 1::2] = words >> 4
        vals = E2M1[nib]
    vals = vals * np.repeat(np.exp2(scales.astype(np.float64) - 127.0), 8, axis=1)[..., None]
    return vals.transpose(0, 1, 3, 2).reshape(g * 512, n)


B, G0, G1, C0, C1, NC = 8, 4, 4, 4096, 6144, 122
NCH = 5 + 1 + NC
STRIDES = [8, 16]
SXY = [1.2, 1.1]
ANCH = [[[10, 13], [16, 30], [33, 23]], [[30, 61], [62, 45], [59, 119]]]
RAD = np.pi / 180.0
ANGLES = [RAD * a for a in (-60.0, -30.0, 0.0, 30.0, 60.0, 90.0)]
NA = len(ANCH[0]) * len(ANGLES)
FMT = "e4m3"


def sigmoid(v):
    return 1.0 / (1.0 + np.exp(-v))


def _masked_anchors(level):
    s = STRIDES[level]
    return np.array([[w / s, h / s, a] for (w, h) in ANCH[level] for a in ANGLES], dtype=np.float64)


def _decode(feat, W, b, level):
    Bn, C, G, _ = feat.shape
    out = (W @ mxq(feat.reshape(Bn, C, G * G), 1, "e4m3")) + b[None, :, None]
    pred = out.reshape(Bn, NA, NCH, G, G).transpose(0, 1, 3, 4, 2)
    sxy = SXY[level]
    s = float(STRIDES[level])
    ma = _masked_anchors(level)
    aw = ma[:, 0][None, :, None, None]
    ah = ma[:, 1][None, :, None, None]
    aa = ma[:, 2][None, :, None, None]
    gx = np.arange(G, dtype=np.float64)[None, None, None, :]
    gy = np.arange(G, dtype=np.float64)[None, None, :, None]
    px = sigmoid(pred[..., 0]) * sxy - (sxy - 1.0) / 2.0 + gx
    py = sigmoid(pred[..., 1]) * sxy - (sxy - 1.0) / 2.0 + gy
    pw = np.exp(pred[..., 2]) * aw
    ph = np.exp(pred[..., 3]) * ah
    pa = pred[..., 4] + aa
    conf = sigmoid(pred[..., 5])
    cls = sigmoid(pred[..., 6:])
    boxes = np.stack([px * s, py * s, pw * s, ph * s, pa], axis=-1)
    out = np.concatenate([boxes, conf[..., None], cls], axis=-1)
    return out.reshape(Bn, -1, NCH)


def _draw_level(G, C):
    s = mx_kscale(C)
    g = np.full(NCH, 1.5)
    g[2:4] = 0.3
    x = np.random.standard_normal((B, C, G, G)) * s[None, :, None, None]
    W = np.random.standard_normal((NA, NCH, C)) * g[None, :, None] / np.sqrt(C) / s
    b = np.random.standard_normal((NA, NCH)) * 0.4
    b[:, 2:4] -= 2.0
    words, scales = pack_weight(np.ascontiguousarray(W.reshape(NA * NCH, C).T), FMT)
    return bf(x), words, scales, bf(b.reshape(NA * NCH))


def setup_inputs():
    x0, W0_words, W0_scales, b0 = _draw_level(G0, C0)
    x1, W1_words, W1_scales, b1 = _draw_level(G1, C1)
    return {"x0": x0, "x1": x1, "W0_words": W0_words, "W0_scales": W0_scales, "b0": b0, "W1_words": W1_words, "W1_scales": W1_scales, "b1": b1}


def reference(x0, x1, W0_words, W0_scales, b0, W1_words, W1_scales, b1):
    o0 = _decode(f64(x0), unpack_weight(W0_words, W0_scales, FMT).T, f64(b0), 0)
    o1 = _decode(f64(x1), unpack_weight(W1_words, W1_scales, FMT).T, f64(b1), 1)
    return np.concatenate([o0, o1], axis=1)

@@ -1,0 +1,159 @@
+from contextlib import ExitStack
+
+import concourse.mybir as mybir
+
+F32 = mybir.dt.float32
+BF16 = mybir.dt.bfloat16
+I32 = mybir.dt.int32
+U8 = mybir.dt.uint8
+U32 = mybir.dt.uint32
+FP8X4 = mybir.dt.float8_e4m3fn_x4
+ALU = mybir.AluOpType
+ACT = mybir.ActivationFunctionType
+
+P = 128
+BATCH = 8
+CELLS = 16
+NA = 18
+NF = 128
+NO = NA * NF
+GROUPS = [8, 12]
+GOFF = [0, 8]
+NGROUPS = 20
+STRIDES = [8.0, 16.0]
+SXY = [1.2, 1.1]
+ANCH = [[[10, 13], [16, 30], [33, 23]], [[30, 61], [62, 45], [59, 119]]]
+ANGLES_DEG = [-60.0, -30.0, 0.0, 30.0, 60.0, 90.0]
+RAD = 3.141592653589793 / 180.0
+CHUNKS = [(0, 512), (512, 512), (1024, 512), (1536, 512), (2048, 256)]
+W_BUFS = 12
+
+FLOPS = 2 * 128 * (4096 + 6144) * NO
+
+
+def tile_detect_w_kernel(tc, x0, x1, W0_words, W0_scales, b0, W1_words, W1_scales, b1, out):
+    nc = tc.nc
+    xs = [x0, x1]
+    words = [W0_words, W1_words]
+    scl = [W0_scales, W1_scales]
+    bs = [b0, b1]
+    with ExitStack() as ctx:
+        keep = ctx.enter_context(tc.tile_pool(name="keep", bufs=1))
+        wpool = ctx.enter_context(tc.tile_pool(name="wpool", bufs=W_BUFS))
+        work = ctx.enter_context(tc.tile_pool(name="work", bufs=3))
+        psum = ctx.enter_context(tc.psum_pool(name="psum", bufs=8))
+
+        planes = keep.tile([P, NGROUPS // 4, NO], U8, name="planes", align_bytes=64)
+        brow = keep.tile([P, 2, NO], BF16, name="brow")
+        ones = keep.tile([P, P], BF16, name="ones")
+        bias_bc = keep.tile([P, 2, NO], F32, name="bias_bc")
+        xcodes = keep.tile([P, NGROUPS, P], U32, name="xcodes", align_bytes=64)
+        xplanes = keep.tile([P, NGROUPS, P], U8, name="xplanes", align_bytes=64)
+        grouped = keep.tile([P, NGROUPS, 4 * P], BF16, name="grouped", align_bytes=64)
+        xraw = [
+            keep.tile([P, BATCH, GROUPS[0], 64], BF16, name="xraw0"),
+            keep.tile([P, BATCH, GROUPS[1], 64], BF16, name="xraw1"),
+        ]
+        pidx = keep.tile([P, 1], I32, name="pidx")
+        gint = keep.tile([P, 2], I32, name="gint")
+        gflt = keep.tile([P, 2], F32, name="gflt")
+        gxy = keep.tile([P, 2, 2], F32, name="gxy")
+        wh = keep.tile([P, 2, NA, 2], F32, name="wh")
+        ang = keep.tile([P, NA], F32, name="ang")
+
+        nc.vector.memset(planes[:].bitcast(I32), 0)
+        nc.vector.memset(brow[:].bitcast(I32), 0)
+        nc.vector.memset(ones[:], 1.0)
+
+        for lv in range(2):
+            src = xs[lv].rearrange("b (g p t) h w -> b p g (t h w)", p=P, t=4)
+            for b in range(BATCH):
+                nc.sync.dma_start(out=xraw[lv][:, b, :, :], in_=src[b])
+        for lv in range(2):
+            nc.scalar.dma_start(out=brow[0:1, lv, :], in_=bs[lv].unsqueeze(0))
+        for lv in range(2):
+            for jj in range(GROUPS[lv] // 4):
+                for q in range(4):
+                    nc.sync.dma_start(
+                        out=planes[32 * q : 32 * q + 16, GOFF[lv] // 4 + jj, :].bitcast(I32),
+                        in_=scl[lv][4 * jj : 4 * jj + 4, 4 * q : 4 * q + 4, :].bitcast(I32),
+                    )
+
+        nc.gpsimd.iota(out=pidx[:], pattern=[[0, 1]], base=0, channel_multiplier=1)
+        nc.vector.tensor_scalar(out=gint[:, 0:1], in0=pidx[:], scalar1=3, scalar2=3,
+                                op0=ALU.logical_shift_right, op1=ALU.bitwise_and)
+        nc.vector.tensor_scalar(out=gint[:, 1:2], in0=pidx[:], scalar1=5, scalar2=3,
+                                op0=ALU.logical_shift_right, op1=ALU.bitwise_and)
+        nc.vector.tensor_copy(out=gflt[:], in_=gint[:])
+        for lv in range(2):
+            st = STRIDES[lv]
+            nc.vector.tensor_scalar(out=gxy[:, lv, :], in0=gflt[:], scalar1=st,
+                                    scalar2=-st * (SXY[lv] - 1.0) / 2.0, op0=ALU.mult, op1=ALU.add)
+            for i in range(3):
+                for d in range(2):
+                    nc.gpsimd.memset(wh[:, lv, 6 * i : 6 * i + 6, d : d + 1], (ANCH[lv][i][d] / st) * st)
+        ang3 = ang[:].rearrange("p (i j) -> p i j", j=6)
+        for j in range(6):
+            nc.gpsimd.memset(ang3[:, :, j : j + 1], RAD * ANGLES_DEG[j])
+
+        for lv in range(2):
+            for (c0, cn) in CHUNKS:
+                bp = psum.tile([P, 512], F32, name="bp", tag="bank")
+                nc.tensor.matmul(out=bp[:, :cn], lhsT=ones[:], rhs=brow[:, lv, c0 : c0 + cn], start=True, stop=True)
+                nc.scalar.copy(out=bias_bc[:, lv, c0 : c0 + cn], in_=bp[:, :cn])
+
+        for lv in range(2):
+            for g in range(GROUPS[lv]):
+                nc.vector.tensor_copy(
+                    out=grouped[:, GOFF[lv] + g, :].rearrange("p (s b t) -> p s b t", s=CELLS, b=BATCH),
+                    in_=xraw[lv][:, :, g, :].rearrange("p b (t s) -> p s b t", t=4),
+                )
+        for (g0, g1) in [(0, 8), (8, 16), (16, 20)]:
+            nc.vector.quantize_mx(
+                out=xcodes[:, g0:g1, :].rearrange("p g m -> p (g m)").bitcast(FP8X4),
+                scales=xplanes[:, g0:g1, :].rearrange("p g m -> p (g m)"),
+                in_=grouped[:, g0:g1, :].rearrange("p g c -> p (g c)"),
+            )
+
+        for lv in range(2):
+            st = STRIDES[lv]
+            acc = [psum.tile([P, 512], F32, name="acc%d_%d" % (lv, j), tag="bank") for j in range(len(CHUNKS))]
+            for g in range(GROUPS[lv]):
+                gg = GOFF[lv] + g
+                wt = wpool.tile([P, 4 * NO], U8, name="wt", align_bytes=64)
+                nc.sync.dma_start(out=wt[:].bitcast(I32),
+                                  in_=words[lv][g].rearrange("p n t -> p (n t)").bitcast(I32))
+                k0 = 4 * (gg % 4)
+                for j, (c0, cn) in enumerate(CHUNKS):
+                    nc.tensor.matmul_mx(
+                        out=acc[j][:, :cn],
+                        lhsT=xcodes[:, gg, :].bitcast(FP8X4),
+                        lhsT_scale=xplanes[:, gg, :],
+                        rhs=wt[:, 4 * c0 : 4 * (c0 + cn)].bitcast(FP8X4),
+                        rhs_scale=planes[k0:P, gg // 4, c0 : c0 + cn],
+                        start=(g == 0),
+                        stop=(g == GROUPS[lv] - 1),
+                    )
+            for j, (c0, cn) in enumerate(CHUNKS):
+                a0 = c0 // NF
+                na = cn // NF
+                pre = work.tile([P, 512], F32, name="pre")
+                res = work.tile([P, 512], F32, name="res")
+                inv = work.tile([P, 4, 2], F32, name="inv")
+                nc.vector.tensor_tensor(out=pre[:, :cn], in0=acc[j][:, :cn], in1=bias_bc[:, lv, c0 : c0 + cn], op=ALU.add)
+                nc.scalar.activation(out=res[:, :cn], in_=pre[:, :cn], func=ACT.Sigmoid)
+                pre3 = pre[:, :cn].rearrange("p (a f) -> p a f", f=NF)
+                res3 = res[:, :cn].rearrange("p (a f) -> p a f", f=NF)
+                nc.scalar.activation(out=inv[:, :na, :], in_=pre3[:, :, 2:4], func=ACT.Sigmoid, scale=-1.0)
+                nc.vector.reciprocal(out=inv[:, :na, :], in_=inv[:, :na, :])
+                nc.vector.tensor_tensor(out=inv[:, :na, :], in0=inv[:, :na, :], in1=wh[:, lv, a0 : a0 + na, :], op=ALU.mult)
+                nc.vector.tensor_tensor(out=res3[:, :, 2:4], in0=res3[:, :, 2:4], in1=inv[:, :na, :], op=ALU.mult)
+                nc.vector.scalar_tensor_tensor(
+                    out=res3[:, :, 0:2], in0=res3[:, :, 0:2], scalar=SXY[lv] * st,
+                    in1=gxy[:, lv, :].unsqueeze(1).to_broadcast([P, na, 2]), op0=ALU.mult, op1=ALU.add)
+                nc.vector.tensor_tensor(out=res3[:, :, 4:5], in0=pre3[:, :, 4:5],
+                                        in1=ang[:, a0 : a0 + na].unsqueeze(2), op=ALU.add)
+                for a in range(na):
+                    r0 = 288 * lv + CELLS * (a0 + a)
+                    eng = nc.gpsimd if lv == 0 else nc.sync
+                    eng.dma_start(out=out[:, r0 : r0 + CELLS, :].rearrange("b s f -> s b f"), in_=res3[:, a, :])

@@ -1,6 +1,8 @@
+import math
 from contextlib import ExitStack
 
 import concourse.mybir as mybir
+from concourse.masks import make_identity
 
 F32 = mybir.dt.float32
 BF16 = mybir.dt.bfloat16
@@ -20,6 +22,7 @@ NO = NA * NF
 GROUPS = [8, 12]
 GOFF = [0, 8]
 NGROUPS = 20
+ROW = 8192
 STRIDES = [8.0, 16.0]
 SXY = [1.2, 1.1]
 ANCH = [[[10, 13], [16, 30], [33, 23]], [[30, 61], [62, 45], [59, 119]]]
@@ -27,133 +30,216 @@ ANGLES_DEG = [-60.0, -30.0, 0.0, 30.0, 60.0, 90.0]
 RAD = 3.141592653589793 / 180.0
 CHUNKS = [(0, 512), (512, 512), (1024, 512), (1536, 512), (2048, 256)]
 W_BUFS = 12
+TAIL_G = [6, 7]
 
 FLOPS = 2 * 128 * (4096 + 6144) * NO
 
 
 def tile_detect_w_kernel(tc, x0, x1, W0_words, W0_scales, b0, W1_words, W1_scales, b1, out):
     nc = tc.nc
-    xs = [x0, x1]
     words = [W0_words, W1_words]
     scl = [W0_scales, W1_scales]
     bs = [b0, b1]
     with ExitStack() as ctx:
+        ctx.enter_context(tc.manual_schedule())
         keep = ctx.enter_context(tc.tile_pool(name="keep", bufs=1))
         wpool = ctx.enter_context(tc.tile_pool(name="wpool", bufs=W_BUFS))
-        work = ctx.enter_context(tc.tile_pool(name="work", bufs=3))
         psum = ctx.enter_context(tc.psum_pool(name="psum", bufs=8))
 
         planes = keep.tile([P, NGROUPS // 4, NO], U8, name="planes", align_bytes=64)
-        brow = keep.tile([P, 2, NO], BF16, name="brow")
-        ones = keep.tile([P, P], BF16, name="ones")
         bias_bc = keep.tile([P, 2, NO], F32, name="bias_bc")
         xcodes = keep.tile([P, NGROUPS, P], U32, name="xcodes", align_bytes=64)
         xplanes = keep.tile([P, NGROUPS, P], U8, name="xplanes", align_bytes=64)
-        grouped = keep.tile([P, NGROUPS, 4 * P], BF16, name="grouped", align_bytes=64)
-        xraw = [
-            keep.tile([P, BATCH, GROUPS[0], 64], BF16, name="xraw0"),
-            keep.tile([P, BATCH, GROUPS[1], 64], BF16, name="xraw1"),
-        ]
         pidx = keep.tile([P, 1], I32, name="pidx")
         gint = keep.tile([P, 2], I32, name="gint")
         gflt = keep.tile([P, 2], F32, name="gflt")
         gxy = keep.tile([P, 2, 2], F32, name="gxy")
-        wh = keep.tile([P, 2, NA, 2], F32, name="wh")
-        ang = keep.tile([P, NA], F32, name="ang")
+        wts = []
+        seq = [(1, g) for g in range(12)] + [(0, g) for g in range(6)]
 
-        nc.vector.memset(planes[:].bitcast(I32), 0)
-        nc.vector.memset(brow[:].bitcast(I32), 0)
-        nc.vector.memset(ones[:], 1.0)
+        def load_w(i):
+            lv, g = seq[i]
+            wt = wpool.tile([P, 4 * NO], U8, name="wt", align_bytes=64)
+            nc.sync.dma_start(out=wt[:].bitcast(I32),
+                              in_=words[lv][g].rearrange("p n t -> p (n t)").bitcast(I32))
+            wts.append(wt)
 
-        for lv in range(2):
-            src = xs[lv].rearrange("b (g p t) h w -> b p g (t h w)", p=P, t=4)
-            for b in range(BATCH):
-                nc.sync.dma_start(out=xraw[lv][:, b, :, :], in_=src[b])
-        for lv in range(2):
-            nc.scalar.dma_start(out=brow[0:1, lv, :], in_=bs[lv].unsqueeze(0))
-        for lv in range(2):
-            for jj in range(GROUPS[lv] // 4):
-                for q in range(4):
-                    nc.sync.dma_start(
-                        out=planes[32 * q : 32 * q + 16, GOFF[lv] // 4 + jj, :].bitcast(I32),
-                        in_=scl[lv][4 * jj : 4 * jj + 4, 4 * q : 4 * q + 4, :].bitcast(I32),
-                    )
-
-        nc.gpsimd.iota(out=pidx[:], pattern=[[0, 1]], base=0, channel_multiplier=1)
-        nc.vector.tensor_scalar(out=gint[:, 0:1], in0=pidx[:], scalar1=3, scalar2=3,
-                                op0=ALU.logical_shift_right, op1=ALU.bitwise_and)
-        nc.vector.tensor_scalar(out=gint[:, 1:2], in0=pidx[:], scalar1=5, scalar2=3,
-                                op0=ALU.logical_shift_right, op1=ALU.bitwise_and)
-        nc.vector.tensor_copy(out=gflt[:], in_=gint[:])
-        for lv in range(2):
-            st = STRIDES[lv]
-            nc.vector.tensor_scalar(out=gxy[:, lv, :], in0=gflt[:], scalar1=st,
-                                    scalar2=-st * (SXY[lv] - 1.0) / 2.0, op0=ALU.mult, op1=ALU.add)
-            for i in range(3):
-                for d in range(2):
-                    nc.gpsimd.memset(wh[:, lv, 6 * i : 6 * i + 6, d : d + 1], (ANCH[lv][i][d] / st) * st)
-        ang3 = ang[:].rearrange("p (i j) -> p i j", j=6)
-        for j in range(6):
-            nc.gpsimd.memset(ang3[:, :, j : j + 1], RAD * ANGLES_DEG[j])
-
-        for lv in range(2):
-            for (c0, cn) in CHUNKS:
-                bp = psum.tile([P, 512], F32, name="bp", tag="bank")
-                nc.tensor.matmul(out=bp[:, :cn], lhsT=ones[:], rhs=brow[:, lv, c0 : c0 + cn], start=True, stop=True)
-                nc.scalar.copy(out=bias_bc[:, lv, c0 : c0 + cn], in_=bp[:, :cn])
-
-        for lv in range(2):
-            for g in range(GROUPS[lv]):
-                nc.vector.tensor_copy(
-                    out=grouped[:, GOFF[lv] + g, :].rearrange("p (s b t) -> p s b t", s=CELLS, b=BATCH),
-                    in_=xraw[lv][:, :, g, :].rearrange("p b (t s) -> p s b t", t=4),
+        def load_planes(j):
+            lv = 0 if j < 2 else 1
+            jj = j - GOFF[lv] // 4
+            for q in range(4):
+                nc.sync.dma_start(
+                    out=planes[32 * q : 32 * q + 16, j, :].bitcast(I32),
+                    in_=scl[lv][4 * jj : 4 * jj + 4, 4 * q : 4 * q + 4, :].bitcast(I32),
                 )
-        for (g0, g1) in [(0, 8), (8, 16), (16, 20)]:
-            nc.vector.quantize_mx(
-                out=xcodes[:, g0:g1, :].rearrange("p g m -> p (g m)").bitcast(FP8X4),
-                scales=xplanes[:, g0:g1, :].rearrange("p g m -> p (g m)"),
-                in_=grouped[:, g0:g1, :].rearrange("p g c -> p (g c)"),
+
+        def passes(acc, j, gg, rhs, first, last):
+            c0, cn = CHUNKS[j]
+            k0 = 4 * (gg % 4)
+            nc.tensor.matmul_mx(
+                out=acc[j][:, :cn],
+                lhsT=xcodes[:, gg, :].bitcast(FP8X4),
+                lhsT_scale=xplanes[:, gg, :],
+                rhs=rhs.bitcast(FP8X4),
+                rhs_scale=planes[k0:P, gg // 4, c0 : c0 + cn],
+                start=first,
+                stop=last,
             )
 
-        for lv in range(2):
-            st = STRIDES[lv]
-            acc = [psum.tile([P, 512], F32, name="acc%d_%d" % (lv, j), tag="bank") for j in range(len(CHUNKS))]
-            for g in range(GROUPS[lv]):
-                gg = GOFF[lv] + g
-                wt = wpool.tile([P, 4 * NO], U8, name="wt", align_bytes=64)
-                nc.sync.dma_start(out=wt[:].bitcast(I32),
-                                  in_=words[lv][g].rearrange("p n t -> p (n t)").bitcast(I32))
-                k0 = 4 * (gg % 4)
-                for j, (c0, cn) in enumerate(CHUNKS):
-                    nc.tensor.matmul_mx(
-                        out=acc[j][:, :cn],
-                        lhsT=xcodes[:, gg, :].bitcast(FP8X4),
-                        lhsT_scale=xplanes[:, gg, :],
-                        rhs=wt[:, 4 * c0 : 4 * (c0 + cn)].bitcast(FP8X4),
-                        rhs_scale=planes[k0:P, gg // 4, c0 : c0 + cn],
-                        start=(g == 0),
-                        stop=(g == GROUPS[lv] - 1),
-                    )
+        with tc.tile_pool(name="prep", bufs=1) as prep:
+            t1 = prep.tile([P, ROW], BF16, name="t1")
+            t2 = prep.tile([P, ROW], BF16, name="t2")
+            grouped = prep.tile([P, NGROUPS, 4 * P], BF16, name="grouped", align_bytes=64)
+            brow = prep.tile([P, 2, NO], BF16, name="brow")
+            ones = prep.tile([P, P], BF16, name="ones")
+            ident = prep.tile([P, P], F32, name="ident")
+
+            nc.vector.memset(t2[:].bitcast(I32), 0)
+            nc.vector.memset(planes[:].bitcast(I32), 0)
+            nc.vector.memset(brow[:].bitcast(I32), 0)
+            nc.vector.memset(ones[:], 1.0)
+            make_identity(nc, ident[:])
+
+            x0v = x0.rearrange("b (g r) h w -> (b g) (r h w)", g=GROUPS[0])
+            x1v = x1.rearrange("b (g r) h w -> (b g) (r h w)", g=GROUPS[1])
+            nc.sync.dma_start(out=t1[0:96, :], in_=x1v)
+            nc.sync.dma_start(out=t1[96:128, :], in_=x0v[0:32])
+            nc.sync.dma_start(out=t2[0:128:4, :], in_=x0v[32:64])
+            for lv in range(2):
+                nc.scalar.dma_start(out=brow[0:1, lv, :], in_=bs[lv].unsqueeze(0))
+            load_planes(2)
+            load_planes(3)
+            for i in range(0, 4):
+                load_w(i)
+            load_planes(4)
+            for i in range(4, 8):
+                load_w(i)
+            load_planes(0)
+            for i in range(8, 12):
+                load_w(i)
+            load_planes(1)
+
+            nc.gpsimd.iota(out=pidx[:], pattern=[[0, 1]], base=0, channel_multiplier=1)
+            nc.vector.tensor_scalar(out=gint[:, 0:1], in0=pidx[:], scalar1=3, scalar2=3,
+                                    op0=ALU.logical_shift_right, op1=ALU.bitwise_and)
+            nc.vector.tensor_scalar(out=gint[:, 1:2], in0=pidx[:], scalar1=5, scalar2=3,
+                                    op0=ALU.logical_shift_right, op1=ALU.bitwise_and)
+            nc.vector.tensor_copy(out=gflt[:], in_=gint[:])
+            for lv in range(2):
+                nc.vector.tensor_scalar(out=gxy[:, lv, :], in0=gflt[:], scalar1=STRIDES[lv],
+                                        scalar2=-STRIDES[lv] * (SXY[lv] - 1.0) / 2.0, op0=ALU.mult, op1=ALU.add)
+
+            g5 = grouped[:].rearrange("p g (s b t) -> p g s b t", s=CELLS, b=BATCH)
+            t1f = t1[:].bitcast(F32)
+            t2f = t2[:].bitcast(F32)
+            for sg in range(8):
+                tp = psum.tile([P, 512], F32, name="tp", tag="bank")
+                for t in range(4):
+                    nc.tensor.transpose(out=tp[:, P * t : P * (t + 1)], in_=t1f[:, 8 * t + sg : ROW // 2 : 32],
+                                        identity=ident[:])
+                tv = tp[:].bitcast(BF16).rearrange("p (t q e) -> p t q e", t=4, e=2)
+                nc.vector.tensor_copy(
+                    out=g5[:, 8:20, 2 * sg : 2 * sg + 2, :, :],
+                    in_=tv[:, :, 0:96, :].rearrange("p t (b g) e -> p g e b t", g=12))
+                nc.vector.tensor_copy(
+                    out=g5[:, 0:8, 2 * sg : 2 * sg + 2, 0:4, :],
+                    in_=tv[:, :, 96:128, :].rearrange("p t (b g) e -> p g e b t", g=8))
+            for (g0, g1) in [(8, 16), (16, 20)]:
+                nc.vector.quantize_mx(
+                    out=xcodes[:, g0:g1, :].rearrange("p g m -> p (g m)").bitcast(FP8X4),
+                    scales=xplanes[:, g0:g1, :].rearrange("p g m -> p (g m)"),
+                    in_=grouped[:, g0:g1, :].rearrange("p g c -> p (g c)"),
+                )
+            for sg in range(8):
+                tq = psum.tile([P, 512], F32, name="tq", tag="bank")
+                for t in range(4):
+                    nc.tensor.transpose(out=tq[:, P * t : P * (t + 1)], in_=t2f[:, 8 * t + sg : ROW // 2 : 32],
+                                        identity=ident[:])
+                tw = tq[:].bitcast(BF16).rearrange("p (t r z e) -> p t r z e", t=4, z=4, e=2)
+                nc.scalar.copy(
+                    out=g5[:, 0:8, 2 * sg : 2 * sg + 2, 4:8, :],
+                    in_=tw[:, :, :, 0, :].rearrange("p t (b g) e -> p g e b t", g=8))
+            nc.vector.quantize_mx(
+                out=xcodes[:, 0:8, :].rearrange("p g m -> p (g m)").bitcast(FP8X4),
+                scales=xplanes[:, 0:8, :].rearrange("p g m -> p (g m)"),
+                in_=grouped[:, 0:8, :].rearrange("p g c -> p (g c)"),
+            )
+            for lv in (1, 0):
+                for (c0, cn) in CHUNKS:
+                    bp = psum.tile([P, 512], F32, name="bp", tag="bank")
+                    nc.tensor.matmul(out=bp[:, :cn], lhsT=ones[:], rhs=brow[:, lv, c0 : c0 + cn], start=True, stop=True)
+                    nc.scalar.copy(out=bias_bc[:, lv, c0 : c0 + cn], in_=bp[:, :cn])
+                bb = bias_bc[:, lv, :].rearrange("p (i j f) -> p i j f", i=3, j=6)
+                for i in range(3):
+                    for d in range(2):
+                        nc.vector.tensor_scalar_add(out=bb[:, i, :, 2 + d : 3 + d], in0=bb[:, i, :, 2 + d : 3 + d],
+                                                    scalar1=math.log((ANCH[lv][i][d] / STRIDES[lv]) * STRIDES[lv]))
+                for j in range(6):
+                    nc.vector.tensor_scalar_add(out=bb[:, :, j, 4:5], in0=bb[:, :, j, 4:5],
+                                                scalar1=RAD * ANGLES_DEG[j])
+
+        resp = ctx.enter_context(tc.tile_pool(name="resp", bufs=10))
+        tmp = ctx.enter_context(tc.tile_pool(name="tmp", bufs=3))
+        late = ctx.enter_context(tc.tile_pool(name="late", bufs=1))
+        wtail = late.tile([P, 2, 4 * NO], U8, name="wtail", align_bytes=64)
+
+        def decode_a(lv, j, acc):
+            c0, cn = CHUNKS[j]
+            na = cn // NF
+            pre = tmp.tile([P, 512], F32, name="pre")
+            inv = tmp.tile([P, 4, 2], F32, name="inv")
+            res = resp.tile([P, 512], F32, name="res")
+            pre3 = pre[:, :cn].rearrange("p (a f) -> p a f", f=NF)
+            nc.vector.tensor_tensor(out=pre[:, :cn], in0=acc[j][:, :cn], in1=bias_bc[:, lv, c0 : c0 + cn], op=ALU.add)
+            nc.scalar.activation(out=inv[:, :na, :], in_=pre3[:, :, 2:4], func=ACT.Sigmoid, scale=-1.0)
+            nc.scalar.activation(out=res[:, :cn], in_=pre[:, :cn], func=ACT.Sigmoid)
+            return (lv, j, pre, inv, res)
+
+        def decode_b(state, eng):
+            lv, j, pre, inv, res = state
+            c0, cn = CHUNKS[j]
+            a0 = c0 // NF
+            na = cn // NF
+            pre3 = pre[:, :cn].rearrange("p (a f) -> p a f", f=NF)
+            res3 = res[:, :cn].rearrange("p (a f) -> p a f", f=NF)
+            nc.vector.reciprocal(out=inv[:, :na, :], in_=inv[:, :na, :])
+            nc.vector.tensor_tensor(out=res3[:, :, 2:4], in0=res3[:, :, 2:4], in1=inv[:, :na, :], op=ALU.mult)
+            nc.vector.scalar_tensor_tensor(
+                out=res3[:, :, 0:2], in0=res3[:, :, 0:2], scalar=SXY[lv] * STRIDES[lv],
+                in1=gxy[:, lv, :].unsqueeze(1).to_broadcast([P, na, 2]), op0=ALU.mult, op1=ALU.add)
+            nc.vector.tensor_copy(out=res3[:, :, 4:5], in_=pre3[:, :, 4:5])
+            for a in range(na):
+                r0 = 288 * lv + CELLS * (a0 + a)
+                eng.dma_start(out=out[:, r0 : r0 + CELLS, :].rearrange("b s f -> s b f"), in_=res3[:, a, :])
+
+        acc = None
+        for i in range(len(seq)):
+            lv, g = seq[i]
+            if g == 0:
+                acc = [psum.tile([P, 512], F32, name="acc%d_%d" % (lv, j), tag="bank") for j in range(len(CHUNKS))]
             for j, (c0, cn) in enumerate(CHUNKS):
-                a0 = c0 // NF
-                na = cn // NF
-                pre = work.tile([P, 512], F32, name="pre")
-                res = work.tile([P, 512], F32, name="res")
-                inv = work.tile([P, 4, 2], F32, name="inv")
-                nc.vector.tensor_tensor(out=pre[:, :cn], in0=acc[j][:, :cn], in1=bias_bc[:, lv, c0 : c0 + cn], op=ALU.add)
-                nc.scalar.activation(out=res[:, :cn], in_=pre[:, :cn], func=ACT.Sigmoid)
-                pre3 = pre[:, :cn].rearrange("p (a f) -> p a f", f=NF)
-                res3 = res[:, :cn].rearrange("p (a f) -> p a f", f=NF)
-                nc.scalar.activation(out=inv[:, :na, :], in_=pre3[:, :, 2:4], func=ACT.Sigmoid, scale=-1.0)
-                nc.vector.reciprocal(out=inv[:, :na, :], in_=inv[:, :na, :])
-                nc.vector.tensor_tensor(out=inv[:, :na, :], in0=inv[:, :na, :], in1=wh[:, lv, a0 : a0 + na, :], op=ALU.mult)
-                nc.vector.tensor_tensor(out=res3[:, :, 2:4], in0=res3[:, :, 2:4], in1=inv[:, :na, :], op=ALU.mult)
-                nc.vector.scalar_tensor_tensor(
-                    out=res3[:, :, 0:2], in0=res3[:, :, 0:2], scalar=SXY[lv] * st,
-                    in1=gxy[:, lv, :].unsqueeze(1).to_broadcast([P, na, 2]), op0=ALU.mult, op1=ALU.add)
-                nc.vector.tensor_tensor(out=res3[:, :, 4:5], in0=pre3[:, :, 4:5],
-                                        in1=ang[:, a0 : a0 + na].unsqueeze(2), op=ALU.add)
-                for a in range(na):
-                    r0 = 288 * lv + CELLS * (a0 + a)
-                    eng = nc.gpsimd if lv == 0 else nc.sync
-                    eng.dma_start(out=out[:, r0 : r0 + CELLS, :].rearrange("b s f -> s b f"), in_=res3[:, a, :])
+                passes(acc, j, GOFF[lv] + g, wts[i][:, 4 * c0 : 4 * (c0 + cn)], g == 0, lv == 1 and g == GROUPS[1] - 1)
+            if i + W_BUFS < len(seq):
+                load_w(i + W_BUFS)
+            if i + W_BUFS == len(seq) - 1:
+                for (c0, cn) in CHUNKS:
+                    nc.sync.dma_start(
+                        out=wtail[:, :, 4 * c0 : 4 * (c0 + cn)].bitcast(I32),
+                        in_=words[0][TAIL_G[0] : TAIL_G[1] + 1, :, c0 : c0 + cn, :].rearrange("g p n t -> p g (n t)").bitcast(I32))
+            if lv == 1 and g == GROUPS[1] - 1:
+                prev = None
+                for j in range(len(CHUNKS)):
+                    cur = decode_a(1, j, acc)
+                    if prev is not None:
+                        decode_b(prev, nc.scalar)
+                    prev = cur
+                decode_b(prev, nc.scalar)
+        prev = None
+        for j, (c0, cn) in enumerate(CHUNKS):
+            for u in range(2):
+                passes(acc, j, GOFF[0] + TAIL_G[u], wtail[:, u, 4 * c0 : 4 * (c0 + cn)], False, u == 1)
+            cur = decode_a(0, j, acc)
+            if prev is not None:
+                decode_b(prev, nc.sync)
+            prev = cur
+        decode_b(prev, nc.sync)

@@ -94,9 +94,9 @@ def tile_detect_w_kernel(tc, x0, x1, W0_words, W0_scales, b0, W1_words, W1_scale
             ones = prep.tile([P, P], BF16, name="ones")
             ident = prep.tile([P, P], F32, name="ident")
 
+            nc.vector.memset(brow[:].bitcast(I32), 0)
             nc.vector.memset(t2[:].bitcast(I32), 0)
             nc.vector.memset(planes[:].bitcast(I32), 0)
-            nc.vector.memset(brow[:].bitcast(I32), 0)
             nc.vector.memset(ones[:], 1.0)
             make_identity(nc, ident[:])
 
@@ -231,9 +231,9 @@ def tile_detect_w_kernel(tc, x0, x1, W0_words, W0_scales, b0, W1_words, W1_scale
                 for j in range(len(CHUNKS)):
                     cur = decode_a(1, j, acc)
                     if prev is not None:
-                        decode_b(prev, nc.scalar)
+                        decode_b(prev, nc.gpsimd)
                     prev = cur
-                decode_b(prev, nc.scalar)
+                decode_b(prev, nc.gpsimd)
         prev = None
         for j, (c0, cn) in enumerate(CHUNKS):
             for u in range(2):

@@ -68,9 +68,9 @@ def tile_detect_w_kernel(tc, x0, x1, W0_words, W0_scales, b0, W1_words, W1_scale
             lv = 0 if j < 2 else 1
             jj = j - GOFF[lv] // 4
             for q in range(4):
-                nc.sync.dma_start(
-                    out=planes[32 * q : 32 * q + 16, j, :].bitcast(I32),
-                    in_=scl[lv][4 * jj : 4 * jj + 4, 4 * q : 4 * q + 4, :].bitcast(I32),
+                nc.gpsimd.dma_start(
+                    out=planes[32 * q : 32 * q + 16, j, :].bitcast(F32),
+                    in_=scl[lv][4 * jj : 4 * jj + 4, 4 * q : 4 * q + 4, :].bitcast(F32),
                 )
 
         def passes(acc, j, gg, rhs, first, last):
@@ -94,9 +94,9 @@ def tile_detect_w_kernel(tc, x0, x1, W0_words, W0_scales, b0, W1_words, W1_scale
             ones = prep.tile([P, P], BF16, name="ones")
             ident = prep.tile([P, P], F32, name="ident")
 
+            nc.vector.memset(planes[:].bitcast(I32), 0)
             nc.vector.memset(brow[:].bitcast(I32), 0)
             nc.vector.memset(t2[:].bitcast(I32), 0)
-            nc.vector.memset(planes[:].bitcast(I32), 0)
             nc.vector.memset(ones[:], 1.0)
             make_identity(nc, ident[:])
 
@@ -107,19 +107,12 @@ def tile_detect_w_kernel(tc, x0, x1, W0_words, W0_scales, b0, W1_words, W1_scale
             nc.sync.dma_start(out=t2[0:128:4, :], in_=x0v[32:64])
             for lv in range(2):
                 nc.scalar.dma_start(out=brow[0:1, lv, :], in_=bs[lv].unsqueeze(0))
-            load_planes(2)
-            load_planes(3)
-            for i in range(0, 4):
+            for i in range(W_BUFS):
                 load_w(i)
-            load_planes(4)
-            for i in range(4, 8):
-                load_w(i)
-            load_planes(0)
-            for i in range(8, 12):
-                load_w(i)
-            load_planes(1)
 
             nc.gpsimd.iota(out=pidx[:], pattern=[[0, 1]], base=0, channel_multiplier=1)
+            for j in (2, 3, 4, 0, 1):
+                load_planes(j)
             nc.vector.tensor_scalar(out=gint[:, 0:1], in0=pidx[:], scalar1=3, scalar2=3,
                                     op0=ALU.logical_shift_right, op1=ALU.bitwise_and)
             nc.vector.tensor_scalar(out=gint[:, 1:2], in0=pidx[:], scalar1=5, scalar2=3,

@@ -30,7 +30,7 @@ ANGLES_DEG = [-60.0, -30.0, 0.0, 30.0, 60.0, 90.0]
 RAD = 3.141592653589793 / 180.0
 CHUNKS = [(0, 512), (512, 512), (1024, 512), (1536, 512), (2048, 256)]
 W_BUFS = 12
-TAIL_G = [6, 7]
+TAIL_G = [10, 11]
 
 FLOPS = 2 * 128 * (4096 + 6144) * NO
 
@@ -55,7 +55,7 @@ def tile_detect_w_kernel(tc, x0, x1, W0_words, W0_scales, b0, W1_words, W1_scale
         gflt = keep.tile([P, 2], F32, name="gflt")
         gxy = keep.tile([P, 2, 2], F32, name="gxy")
         wts = []
-        seq = [(1, g) for g in range(12)] + [(0, g) for g in range(6)]
+        seq = [(0, g) for g in range(8)] + [(1, g) for g in range(10)]
 
         def load_w(i):
             lv, g = seq[i]
@@ -102,16 +102,16 @@ def tile_detect_w_kernel(tc, x0, x1, W0_words, W0_scales, b0, W1_words, W1_scale
 
             x0v = x0.rearrange("b (g r) h w -> (b g) (r h w)", g=GROUPS[0])
             x1v = x1.rearrange("b (g r) h w -> (b g) (r h w)", g=GROUPS[1])
-            nc.sync.dma_start(out=t1[0:96, :], in_=x1v)
-            nc.sync.dma_start(out=t1[96:128, :], in_=x0v[0:32])
-            nc.sync.dma_start(out=t2[0:128:4, :], in_=x0v[32:64])
+            nc.sync.dma_start(out=t1[0:128:2, :], in_=x0v)
+            nc.sync.dma_start(out=t1[1:128:2, :], in_=x1v[0:64])
+            nc.sync.dma_start(out=t2[0:128:4, :], in_=x1v[64:96])
             for lv in range(2):
                 nc.scalar.dma_start(out=brow[0:1, lv, :], in_=bs[lv].unsqueeze(0))
             for i in range(W_BUFS):
                 load_w(i)
 
             nc.gpsimd.iota(out=pidx[:], pattern=[[0, 1]], base=0, channel_multiplier=1)
-            for j in (2, 3, 4, 0, 1):
+            for j in range(NGROUPS // 4):
                 load_planes(j)
             nc.vector.tensor_scalar(out=gint[:, 0:1], in0=pidx[:], scalar1=3, scalar2=3,
                                     op0=ALU.logical_shift_right, op1=ALU.bitwise_and)
@@ -125,39 +125,44 @@ def tile_detect_w_kernel(tc, x0, x1, W0_words, W0_scales, b0, W1_words, W1_scale
             g5 = grouped[:].rearrange("p g (s b t) -> p g s b t", s=CELLS, b=BATCH)
             t1f = t1[:].bitcast(F32)
             t2f = t2[:].bitcast(F32)
-            for sg in range(8):
-                tp = psum.tile([P, 512], F32, name="tp", tag="bank")
-                for t in range(4):
-                    nc.tensor.transpose(out=tp[:, P * t : P * (t + 1)], in_=t1f[:, 8 * t + sg : ROW // 2 : 32],
-                                        identity=ident[:])
-                tv = tp[:].bitcast(BF16).rearrange("p (t q e) -> p t q e", t=4, e=2)
-                nc.vector.tensor_copy(
-                    out=g5[:, 8:20, 2 * sg : 2 * sg + 2, :, :],
-                    in_=tv[:, :, 0:96, :].rearrange("p t (b g) e -> p g e b t", g=12))
-                nc.vector.tensor_copy(
-                    out=g5[:, 0:8, 2 * sg : 2 * sg + 2, 0:4, :],
-                    in_=tv[:, :, 96:128, :].rearrange("p t (b g) e -> p g e b t", g=8))
-            for (g0, g1) in [(8, 16), (16, 20)]:
+            def copier(sg):
+                return nc.vector.tensor_copy if sg % 2 == 0 else nc.scalar.copy
+
+            def quantise(g0, g1):
                 nc.vector.quantize_mx(
                     out=xcodes[:, g0:g1, :].rearrange("p g m -> p (g m)").bitcast(FP8X4),
                     scales=xplanes[:, g0:g1, :].rearrange("p g m -> p (g m)"),
                     in_=grouped[:, g0:g1, :].rearrange("p g c -> p (g c)"),
                 )
+
+            for sg in range(8):
+                tp = psum.tile([P, 512], F32, name="tp", tag="bank")
+                for t in range(4):
+                    nc.tensor.transpose(out=tp[:, P * t : P * (t + 1)], in_=t1f[:, 8 * t + sg : ROW // 2 : 32],
+                                        identity=ident[:])
+                tv = tp[:].bitcast(BF16).rearrange("p (t q z e) -> p t q z e", t=4, z=2, e=2)
+                cells = slice(2 * sg, 2 * sg + 2)
+                copier(sg)(out=g5[:, 0:8, cells, :, :],
+                           in_=tv[:, :, :, 0, :].rearrange("p t (b g) e -> p g e b t", g=8))
+                copier(sg)(out=g5[:, 8:20, cells, 0:5, :],
+                           in_=tv[:, :, 0:60, 1, :].rearrange("p t (b g) e -> p g e b t", g=12))
+                copier(sg)(out=g5[:, 8:12, cells, 5, :],
+                           in_=tv[:, :, 60:64, 1, :].rearrange("p t g e -> p g e t"))
+            quantise(0, 8)
             for sg in range(8):
                 tq = psum.tile([P, 512], F32, name="tq", tag="bank")
                 for t in range(4):
                     nc.tensor.transpose(out=tq[:, P * t : P * (t + 1)], in_=t2f[:, 8 * t + sg : ROW // 2 : 32],
                                         identity=ident[:])
                 tw = tq[:].bitcast(BF16).rearrange("p (t r z e) -> p t r z e", t=4, z=4, e=2)
-                nc.scalar.copy(
-                    out=g5[:, 0:8, 2 * sg : 2 * sg + 2, 4:8, :],
-                    in_=tw[:, :, :, 0, :].rearrange("p t (b g) e -> p g e b t", g=8))
-            nc.vector.quantize_mx(
-                out=xcodes[:, 0:8, :].rearrange("p g m -> p (g m)").bitcast(FP8X4),
-                scales=xplanes[:, 0:8, :].rearrange("p g m -> p (g m)"),
-                in_=grouped[:, 0:8, :].rearrange("p g c -> p (g c)"),
-            )
-            for lv in (1, 0):
+                cells = slice(2 * sg, 2 * sg + 2)
+                copier(sg)(out=g5[:, 12:20, cells, 5, :],
+                           in_=tw[:, :, 0:8, 0, :].rearrange("p t g e -> p g e t"))
+                copier(sg)(out=g5[:, 8:20, cells, 6:8, :],
+                           in_=tw[:, :, 8:32, 0, :].rearrange("p t (b g) e -> p g e b t", g=12))
+            quantise(8, 16)
+            quantise(16, 20)
+            for lv in (0, 1):
                 for (c0, cn) in CHUNKS:
                     bp = psum.tile([P, 512], F32, name="bp", tag="bank")
                     nc.tensor.matmul(out=bp[:, :cn], lhsT=ones[:], rhs=brow[:, lv, c0 : c0 + cn], start=True, stop=True)
@@ -211,18 +216,18 @@ def tile_detect_w_kernel(tc, x0, x1, W0_words, W0_scales, b0, W1_words, W1_scale
             if g == 0:
                 acc = [psum.tile([P, 512], F32, name="acc%d_%d" % (lv, j), tag="bank") for j in range(len(CHUNKS))]
             for j, (c0, cn) in enumerate(CHUNKS):
-                passes(acc, j, GOFF[lv] + g, wts[i][:, 4 * c0 : 4 * (c0 + cn)], g == 0, lv == 1 and g == GROUPS[1] - 1)
+                passes(acc, j, GOFF[lv] + g, wts[i][:, 4 * c0 : 4 * (c0 + cn)], g == 0, lv == 0 and g == GROUPS[0] - 1)
             if i + W_BUFS < len(seq):
                 load_w(i + W_BUFS)
             if i + W_BUFS == len(seq) - 1:
                 for (c0, cn) in CHUNKS:
                     nc.sync.dma_start(
                         out=wtail[:, :, 4 * c0 : 4 * (c0 + cn)].bitcast(I32),
-                        in_=words[0][TAIL_G[0] : TAIL_G[1] + 1, :, c0 : c0 + cn, :].rearrange("g p n t -> p g (n t)").bitcast(I32))
-            if lv == 1 and g == GROUPS[1] - 1:
+                        in_=words[1][TAIL_G[0] : TAIL_G[1] + 1, :, c0 : c0 + cn, :].rearrange("g p n t -> p g (n t)").bitcast(I32))
+            if lv == 0 and g == GROUPS[0] - 1:
                 prev = None
                 for j in range(len(CHUNKS)):
-                    cur = decode_a(1, j, acc)
+                    cur = decode_a(0, j, acc)
                     if prev is not None:
                         decode_b(prev, nc.gpsimd)
                     prev = cur
@@ -230,8 +235,8 @@ def tile_detect_w_kernel(tc, x0, x1, W0_words, W0_scales, b0, W1_words, W1_scale
         prev = None
         for j, (c0, cn) in enumerate(CHUNKS):
             for u in range(2):
-                passes(acc, j, GOFF[0] + TAIL_G[u], wtail[:, u, 4 * c0 : 4 * (c0 + cn)], False, u == 1)
-            cur = decode_a(0, j, acc)
+                passes(acc, j, GOFF[1] + TAIL_G[u], wtail[:, u, 4 * c0 : 4 * (c0 + cn)], False, u == 1)
+            cur = decode_a(1, j, acc)
             if prev is not None:
                 decode_b(prev, nc.sync)
             prev = cur

@@ -67,7 +67,7 @@ def tile_detect_w_kernel(tc, x0, x1, W0_words, W0_scales, b0, W1_words, W1_scale
         def load_planes(j):
             lv = 0 if j < 2 else 1
             jj = j - GOFF[lv] // 4
-            for q in range(4):
+            for q in (0, 2, 1, 3):
                 nc.gpsimd.dma_start(
                     out=planes[32 * q : 32 * q + 16, j, :].bitcast(F32),
                     in_=scl[lv][4 * jj : 4 * jj + 4, 4 * q : 4 * q + 4, :].bitcast(F32),
@@ -94,23 +94,25 @@ def tile_detect_w_kernel(tc, x0, x1, W0_words, W0_scales, b0, W1_words, W1_scale
             ones = prep.tile([P, P], BF16, name="ones")
             ident = prep.tile([P, P], F32, name="ident")
 
+            nc.vector.memset(t2[:].bitcast(I32), 0)
             nc.vector.memset(planes[:].bitcast(I32), 0)
             nc.vector.memset(brow[:].bitcast(I32), 0)
-            nc.vector.memset(t2[:].bitcast(I32), 0)
             nc.vector.memset(ones[:], 1.0)
             make_identity(nc, ident[:])
+            nc.gpsimd.iota(out=pidx[:], pattern=[[0, 1]], base=0, channel_multiplier=1)
 
             x0v = x0.rearrange("b (g r) h w -> (b g) (r h w)", g=GROUPS[0])
             x1v = x1.rearrange("b (g r) h w -> (b g) (r h w)", g=GROUPS[1])
             nc.sync.dma_start(out=t1[0:128:2, :], in_=x0v)
             nc.sync.dma_start(out=t1[1:128:2, :], in_=x1v[0:64])
-            nc.sync.dma_start(out=t2[0:128:4, :], in_=x1v[64:96])
+            for h in (0, 2, 1, 3):
+                nc.gpsimd.dma_start(out=t2[32 * h : 32 * h + 32 : 4, :].bitcast(F32),
+                                    in_=x1v[64 + 8 * h : 72 + 8 * h].bitcast(F32))
             for lv in range(2):
                 nc.scalar.dma_start(out=brow[0:1, lv, :], in_=bs[lv].unsqueeze(0))
             for i in range(W_BUFS):
                 load_w(i)
 
-            nc.gpsimd.iota(out=pidx[:], pattern=[[0, 1]], base=0, channel_multiplier=1)
             for j in range(NGROUPS // 4):
                 load_planes(j)
             nc.vector.tensor_scalar(out=gint[:, 0:1], in0=pidx[:], scalar1=3, scalar2=3,
@@ -238,6 +240,6 @@ def tile_detect_w_kernel(tc, x0, x1, W0_words, W0_scales, b0, W1_words, W1_scale
                 passes(acc, j, GOFF[1] + TAIL_G[u], wtail[:, u, 4 * c0 : 4 * (c0 + cn)], False, u == 1)
             cur = decode_a(1, j, acc)
             if prev is not None:
-                decode_b(prev, nc.sync)
+                decode_b(prev, nc.gpsimd if j == 1 else nc.sync)
             prev = cur
         decode_b(prev, nc.sync)

@@ -67,7 +67,7 @@ def tile_detect_w_kernel(tc, x0, x1, W0_words, W0_scales, b0, W1_words, W1_scale
         def load_planes(j):
             lv = 0 if j < 2 else 1
             jj = j - GOFF[lv] // 4
-            for q in (0, 2, 1, 3):
+            for q in range(4):
                 nc.gpsimd.dma_start(
                     out=planes[32 * q : 32 * q + 16, j, :].bitcast(F32),
                     in_=scl[lv][4 * jj : 4 * jj + 4, 4 * q : 4 * q + 4, :].bitcast(F32),
@@ -86,6 +86,18 @@ def tile_detect_w_kernel(tc, x0, x1, W0_words, W0_scales, b0, W1_words, W1_scale
                 stop=last,
             )
 
+        accs = [None, None]
+
+        def mx_group(i):
+            lv, g = seq[i]
+            if g == 0:
+                accs[lv] = [psum.tile([P, 512], F32, name="acc%d_%d" % (lv, j), tag="bank") for j in range(len(CHUNKS))]
+            for j, (c0, cn) in enumerate(CHUNKS):
+                passes(accs[lv], j, GOFF[lv] + g, wts[i][:, 4 * c0 : 4 * (c0 + cn)], g == 0,
+                       lv == 0 and g == GROUPS[0] - 1)
+            if i + W_BUFS < len(seq):
+                load_w(i + W_BUFS)
+
         with tc.tile_pool(name="prep", bufs=1) as prep:
             t1 = prep.tile([P, ROW], BF16, name="t1")
             t2 = prep.tile([P, ROW], BF16, name="t2")
@@ -94,25 +106,23 @@ def tile_detect_w_kernel(tc, x0, x1, W0_words, W0_scales, b0, W1_words, W1_scale
             ones = prep.tile([P, P], BF16, name="ones")
             ident = prep.tile([P, P], F32, name="ident")
 
-            nc.vector.memset(t2[:].bitcast(I32), 0)
             nc.vector.memset(planes[:].bitcast(I32), 0)
             nc.vector.memset(brow[:].bitcast(I32), 0)
+            nc.vector.memset(t2[:].bitcast(I32), 0)
             nc.vector.memset(ones[:], 1.0)
             make_identity(nc, ident[:])
-            nc.gpsimd.iota(out=pidx[:], pattern=[[0, 1]], base=0, channel_multiplier=1)
 
             x0v = x0.rearrange("b (g r) h w -> (b g) (r h w)", g=GROUPS[0])
             x1v = x1.rearrange("b (g r) h w -> (b g) (r h w)", g=GROUPS[1])
             nc.sync.dma_start(out=t1[0:128:2, :], in_=x0v)
             nc.sync.dma_start(out=t1[1:128:2, :], in_=x1v[0:64])
-            for h in (0, 2, 1, 3):
-                nc.gpsimd.dma_start(out=t2[32 * h : 32 * h + 32 : 4, :].bitcast(F32),
-                                    in_=x1v[64 + 8 * h : 72 + 8 * h].bitcast(F32))
+            nc.sync.dma_start(out=t2[0:128:4, :], in_=x1v[64:96])
             for lv in range(2):
                 nc.scalar.dma_start(out=brow[0:1, lv, :], in_=bs[lv].unsqueeze(0))
             for i in range(W_BUFS):
                 load_w(i)
 
+            nc.gpsimd.iota(out=pidx[:], pattern=[[0, 1]], base=0, channel_multiplier=1)
             for j in range(NGROUPS // 4):
                 load_planes(j)
             nc.vector.tensor_scalar(out=gint[:, 0:1], in0=pidx[:], scalar1=3, scalar2=3,
@@ -151,7 +161,8 @@ def tile_detect_w_kernel(tc, x0, x1, W0_words, W0_scales, b0, W1_words, W1_scale
                 copier(sg)(out=g5[:, 8:12, cells, 5, :],
                            in_=tv[:, :, 60:64, 1, :].rearrange("p t g e -> p g e t"))
             quantise(0, 8)
-            for sg in range(8):
+
+            def second_tile(sg):
                 tq = psum.tile([P, 512], F32, name="tq", tag="bank")
                 for t in range(4):
                     nc.tensor.transpose(out=tq[:, P * t : P * (t + 1)], in_=t2f[:, 8 * t + sg : ROW // 2 : 32],
@@ -162,8 +173,19 @@ def tile_detect_w_kernel(tc, x0, x1, W0_words, W0_scales, b0, W1_words, W1_scale
                            in_=tw[:, :, 0:8, 0, :].rearrange("p t g e -> p g e t"))
                 copier(sg)(out=g5[:, 8:20, cells, 6:8, :],
                            in_=tw[:, :, 8:32, 0, :].rearrange("p t (b g) e -> p g e b t", g=12))
+
+            mx_group(0)
+            mx_group(1)
+            for sg in range(0, 4):
+                second_tile(sg)
+            mx_group(2)
+            mx_group(3)
+            for sg in range(4, 8):
+                second_tile(sg)
             quantise(8, 16)
             quantise(16, 20)
+            mx_group(4)
+            mx_group(5)
             for lv in (0, 1):
                 for (c0, cn) in CHUNKS:
                     bp = psum.tile([P, 512], F32, name="bp", tag="bank")
@@ -212,34 +234,27 @@ def tile_detect_w_kernel(tc, x0, x1, W0_words, W0_scales, b0, W1_words, W1_scale
                 r0 = 288 * lv + CELLS * (a0 + a)
                 eng.dma_start(out=out[:, r0 : r0 + CELLS, :].rearrange("b s f -> s b f"), in_=res3[:, a, :])
 
-        acc = None
-        for i in range(len(seq)):
-            lv, g = seq[i]
-            if g == 0:
-                acc = [psum.tile([P, 512], F32, name="acc%d_%d" % (lv, j), tag="bank") for j in range(len(CHUNKS))]
-            for j, (c0, cn) in enumerate(CHUNKS):
-                passes(acc, j, GOFF[lv] + g, wts[i][:, 4 * c0 : 4 * (c0 + cn)], g == 0, lv == 0 and g == GROUPS[0] - 1)
-            if i + W_BUFS < len(seq):
-                load_w(i + W_BUFS)
-            if i + W_BUFS == len(seq) - 1:
-                for (c0, cn) in CHUNKS:
-                    nc.sync.dma_start(
-                        out=wtail[:, :, 4 * c0 : 4 * (c0 + cn)].bitcast(I32),
-                        in_=words[1][TAIL_G[0] : TAIL_G[1] + 1, :, c0 : c0 + cn, :].rearrange("g p n t -> p g (n t)").bitcast(I32))
-            if lv == 0 and g == GROUPS[0] - 1:
-                prev = None
-                for j in range(len(CHUNKS)):
-                    cur = decode_a(0, j, acc)
-                    if prev is not None:
-                        decode_b(prev, nc.gpsimd)
-                    prev = cur
+        for (c0, cn) in CHUNKS:
+            nc.sync.dma_start(
+                out=wtail[:, :, 4 * c0 : 4 * (c0 + cn)].bitcast(I32),
+                in_=words[1][TAIL_G[0] : TAIL_G[1] + 1, :, c0 : c0 + cn, :].rearrange("g p n t -> p g (n t)").bitcast(I32))
+        mx_group(6)
+        mx_group(7)
+        prev = None
+        for j in range(len(CHUNKS)):
+            cur = decode_a(0, j, accs[0])
+            if prev is not None:
                 decode_b(prev, nc.gpsimd)
+            prev = cur
+        decode_b(prev, nc.gpsimd)
+        for i in range(8, len(seq)):
+            mx_group(i)
         prev = None
         for j, (c0, cn) in enumerate(CHUNKS):
             for u in range(2):
-                passes(acc, j, GOFF[1] + TAIL_G[u], wtail[:, u, 4 * c0 : 4 * (c0 + cn)], False, u == 1)
-            cur = decode_a(1, j, acc)
+                passes(accs[1], j, GOFF[1] + TAIL_G[u], wtail[:, u, 4 * c0 : 4 * (c0 + cn)], False, u == 1)
+            cur = decode_a(1, j, accs[1])
             if prev is not None:
-                decode_b(prev, nc.gpsimd if j == 1 else nc.sync)
+                decode_b(prev, nc.sync)
             prev = cur
         decode_b(prev, nc.sync)

@@ -116,10 +116,12 @@ def tile_detect_w_kernel(tc, x0, x1, W0_words, W0_scales, b0, W1_words, W1_scale
             x1v = x1.rearrange("b (g r) h w -> (b g) (r h w)", g=GROUPS[1])
             nc.sync.dma_start(out=t1[0:128:2, :], in_=x0v)
             nc.sync.dma_start(out=t1[1:128:2, :], in_=x1v[0:64])
-            nc.sync.dma_start(out=t2[0:128:4, :], in_=x1v[64:96])
             for lv in range(2):
                 nc.scalar.dma_start(out=brow[0:1, lv, :], in_=bs[lv].unsqueeze(0))
-            for i in range(W_BUFS):
+            for i in range(2):
+                load_w(i)
+            nc.sync.dma_start(out=t2[0:128:4, :], in_=x1v[64:96])
+            for i in range(2, W_BUFS):
                 load_w(i)
 
             nc.gpsimd.iota(out=pidx[:], pattern=[[0, 1]], base=0, channel_multiplier=1)

@@ -15,7 +15,6 @@ ACT = mybir.ActivationFunctionType
 
 P = 128
 BATCH = 8
-CELLS = 16
 NA = 18
 NF = 128
 NO = NA * NF
@@ -26,9 +25,8 @@ ROW = 8192
 STRIDES = [8.0, 16.0]
 SXY = [1.2, 1.1]
 ANCH = [[[10, 13], [16, 30], [33, 23]], [[30, 61], [62, 45], [59, 119]]]
-ANGLES_DEG = [-60.0, -30.0, 0.0, 30.0, 60.0, 90.0]
 RAD = 3.141592653589793 / 180.0
-CHUNKS = [(0, 512), (512, 512), (1024, 512), (1536, 512), (2048, 256)]
+CHUNKS = [(0, 4), (4, 4), (8, 4), (12, 4), (16, 2)]
 W_BUFS = 12
 TAIL_G = [10, 11]
 
@@ -47,13 +45,18 @@ def tile_detect_w_kernel(tc, x0, x1, W0_words, W0_scales, b0, W1_words, W1_scale
         psum = ctx.enter_context(tc.psum_pool(name="psum", bufs=8))
 
         planes = keep.tile([P, NGROUPS // 4, NO], U8, name="planes", align_bytes=64)
-        bias_bc = keep.tile([P, 2, NO], F32, name="bias_bc")
         xcodes = keep.tile([P, NGROUPS, P], U32, name="xcodes", align_bytes=64)
         xplanes = keep.tile([P, NGROUPS, P], U8, name="xplanes", align_bytes=64)
-        pidx = keep.tile([P, 1], I32, name="pidx")
-        gint = keep.tile([P, 2], I32, name="gint")
-        gflt = keep.tile([P, 2], F32, name="gflt")
-        gxy = keep.tile([P, 2, 2], F32, name="gxy")
+        ident = keep.tile([P, P], F32, name="ident")
+        bcol = keep.tile([P, 64], F32, name="bcol")
+        pint = keep.tile([P, 1], I32, name="pint")
+        xint = keep.tile([P, 4], I32, name="xint")
+        gint = keep.tile([P, 3], I32, name="gint")
+        gflt = keep.tile([P, 3], F32, name="gflt")
+        xflt = keep.tile([P, 4], F32, name="xflt")
+        ge = keep.tile([P, 2], F32, name="ge")
+        grid4 = keep.tile([P, 2, 4, 2], F32, name="grid4")
+        grid1 = keep.tile([P, 2, 2], F32, name="grid1")
         wts = []
         seq = [(0, g) for g in range(8)] + [(1, g) for g in range(10)]
 
@@ -73,18 +76,20 @@ def tile_detect_w_kernel(tc, x0, x1, W0_words, W0_scales, b0, W1_words, W1_scale
                     in_=scl[lv][4 * jj : 4 * jj + 4, 4 * q : 4 * q + 4, :].bitcast(F32),
                 )
 
-        def passes(acc, j, gg, rhs, first, last):
-            c0, cn = CHUNKS[j]
+        def passes(acc, j, gg, wcols, first, last):
+            a0, na = CHUNKS[j]
             k0 = 4 * (gg % 4)
-            nc.tensor.matmul_mx(
-                out=acc[j][:, :cn],
-                lhsT=xcodes[:, gg, :].bitcast(FP8X4),
-                lhsT_scale=xplanes[:, gg, :],
-                rhs=rhs.bitcast(FP8X4),
-                rhs_scale=planes[k0:P, gg // 4, c0 : c0 + cn],
-                start=first,
-                stop=last,
-            )
+            for a in range(na):
+                c = P * (a0 + a)
+                nc.tensor.matmul_mx(
+                    out=acc[j][:, P * a : P * (a + 1)],
+                    lhsT=wcols[:, 4 * P * a : 4 * P * (a + 1)].bitcast(FP8X4),
+                    lhsT_scale=planes[k0:P, gg // 4, c : c + P],
+                    rhs=xcodes[:, gg, :].bitcast(FP8X4),
+                    rhs_scale=xplanes[:, gg, :],
+                    start=first and a == 0,
+                    stop=last and a == na - 1,
+                )
 
         accs = [None, None]
 
@@ -92,8 +97,8 @@ def tile_detect_w_kernel(tc, x0, x1, W0_words, W0_scales, b0, W1_words, W1_scale
             lv, g = seq[i]
             if g == 0:
                 accs[lv] = [psum.tile([P, 512], F32, name="acc%d_%d" % (lv, j), tag="bank") for j in range(len(CHUNKS))]
-            for j, (c0, cn) in enumerate(CHUNKS):
-                passes(accs[lv], j, GOFF[lv] + g, wts[i][:, 4 * c0 : 4 * (c0 + cn)], g == 0,
+            for j, (a0, na) in enumerate(CHUNKS):
+                passes(accs[lv], j, GOFF[lv] + g, wts[i][:, 4 * P * a0 : 4 * P * (a0 + na)], g == 0,
                        lv == 0 and g == GROUPS[0] - 1)
             if i + W_BUFS < len(seq):
                 load_w(i + W_BUFS)
@@ -102,14 +107,12 @@ def tile_detect_w_kernel(tc, x0, x1, W0_words, W0_scales, b0, W1_words, W1_scale
             t1 = prep.tile([P, ROW], BF16, name="t1")
             t2 = prep.tile([P, ROW], BF16, name="t2")
             grouped = prep.tile([P, NGROUPS, 4 * P], BF16, name="grouped", align_bytes=64)
-            brow = prep.tile([P, 2, NO], BF16, name="brow")
-            ones = prep.tile([P, P], BF16, name="ones")
-            ident = prep.tile([P, P], F32, name="ident")
+            brow = prep.tile([P, NF], BF16, name="brow")
+            bf = prep.tile([P, NF], F32, name="bf")
 
+            nc.vector.memset(brow[:], 0.0)
             nc.vector.memset(planes[:].bitcast(I32), 0)
-            nc.vector.memset(brow[:].bitcast(I32), 0)
             nc.vector.memset(t2[:].bitcast(I32), 0)
-            nc.vector.memset(ones[:], 1.0)
             make_identity(nc, ident[:])
 
             x0v = x0.rearrange("b (g r) h w -> (b g) (r h w)", g=GROUPS[0])
@@ -117,28 +120,55 @@ def tile_detect_w_kernel(tc, x0, x1, W0_words, W0_scales, b0, W1_words, W1_scale
             nc.sync.dma_start(out=t1[0:128:2, :], in_=x0v)
             nc.sync.dma_start(out=t1[1:128:2, :], in_=x1v[0:64])
             for lv in range(2):
-                nc.scalar.dma_start(out=brow[0:1, lv, :], in_=bs[lv].unsqueeze(0))
+                nc.scalar.dma_start(out=brow[32 * lv : 32 * lv + NA, :], in_=bs[lv].rearrange("(a f) -> a f", f=NF))
             for i in range(2):
                 load_w(i)
             nc.sync.dma_start(out=t2[0:128:4, :], in_=x1v[64:96])
             for i in range(2, W_BUFS):
                 load_w(i)
 
-            nc.gpsimd.iota(out=pidx[:], pattern=[[0, 1]], base=0, channel_multiplier=1)
+            nc.gpsimd.iota(out=pint[:], pattern=[[0, 1]], base=0, channel_multiplier=1)
+            nc.gpsimd.iota(out=xint[:], pattern=[[1, 4]], base=0, channel_multiplier=0)
             for j in range(NGROUPS // 4):
                 load_planes(j)
-            nc.vector.tensor_scalar(out=gint[:, 0:1], in0=pidx[:], scalar1=3, scalar2=3,
-                                    op0=ALU.logical_shift_right, op1=ALU.bitwise_and)
-            nc.vector.tensor_scalar(out=gint[:, 1:2], in0=pidx[:], scalar1=5, scalar2=3,
-                                    op0=ALU.logical_shift_right, op1=ALU.bitwise_and)
-            nc.vector.tensor_copy(out=gflt[:], in_=gint[:])
-            for lv in range(2):
-                nc.vector.tensor_scalar(out=gxy[:, lv, :], in0=gflt[:], scalar1=STRIDES[lv],
-                                        scalar2=-STRIDES[lv] * (SXY[lv] - 1.0) / 2.0, op0=ALU.mult, op1=ALU.add)
 
-            g5 = grouped[:].rearrange("p g (s b t) -> p g s b t", s=CELLS, b=BATCH)
+            nc.vector.tensor_scalar(out=gint[:, 0:1], in0=pint[:], scalar1=3, scalar2=3,
+                                    op0=ALU.logical_shift_right, op1=ALU.bitwise_and)
+            nc.vector.tensor_scalar(out=gint[:, 1:2], in0=pint[:], scalar1=5, scalar2=3,
+                                    op0=ALU.logical_shift_right, op1=ALU.bitwise_and)
+            nc.vector.tensor_scalar(out=gint[:, 2:3], in0=pint[:], scalar1=31, scalar2=None, op0=ALU.bitwise_and)
+            nc.vector.tensor_copy(out=gflt[:], in_=gint[:])
+            nc.vector.tensor_copy(out=xflt[:], in_=xint[:])
+            for lv in range(2):
+                s = STRIDES[lv]
+                off = -s * (SXY[lv] - 1.0) / 2.0
+                nc.vector.tensor_scalar(out=grid4[:, lv, :, 0], in0=xflt[:], scalar1=s, scalar2=off, op0=ALU.mult, op1=ALU.add)
+                nc.vector.tensor_scalar(out=grid4[:, lv, :, 1], in0=gflt[:, 0:1].to_broadcast([P, 4]), scalar1=s, scalar2=off,
+                                        op0=ALU.mult, op1=ALU.add)
+                nc.vector.tensor_scalar(out=grid1[:, lv, :], in0=gflt[:, 0:2], scalar1=s, scalar2=off, op0=ALU.mult, op1=ALU.add)
+            nc.vector.tensor_copy(out=bf[:], in_=brow[:])
+            nc.vector.tensor_scalar(out=ge[:, 0:1], in0=gflt[:, 2:3], scalar1=5.5, scalar2=None, op0=ALU.is_ge)
+            nc.vector.tensor_scalar(out=ge[:, 1:2], in0=gflt[:, 2:3], scalar1=11.5, scalar2=None, op0=ALU.is_ge)
+            for lv in range(2):
+                rows = slice(32 * lv, 32 * lv + 32)
+                for d in range(2):
+                    sizes = [math.log((ANCH[lv][i][d] / STRIDES[lv]) * STRIDES[lv]) for i in range(3)]
+                    col = bf[rows, 2 + d : 3 + d]
+                    nc.vector.tensor_scalar_add(out=col, in0=col, scalar1=sizes[0])
+                    for i in range(2):
+                        nc.vector.scalar_tensor_tensor(out=col, in0=ge[rows, i : i + 1], scalar=sizes[i + 1] - sizes[i],
+                                                       in1=col, op0=ALU.mult, op1=ALU.add)
+            col = bf[:, 4:5]
+            nc.vector.tensor_scalar_add(out=col, in0=col, scalar1=-60.0 * RAD)
+            nc.vector.scalar_tensor_tensor(out=col, in0=gflt[:, 2:3], scalar=30.0 * RAD, in1=col, op0=ALU.mult, op1=ALU.add)
+            for i in range(2):
+                nc.vector.scalar_tensor_tensor(out=col, in0=ge[:, i : i + 1], scalar=-180.0 * RAD, in1=col,
+                                               op0=ALU.mult, op1=ALU.add)
+
+            g6 = grouped[:].rearrange("p g (x y b t) -> p g x y b t", x=4, y=4, b=BATCH)
             t1f = t1[:].bitcast(F32)
             t2f = t2[:].bitcast(F32)
+
             def copier(sg):
                 return nc.vector.tensor_copy if sg % 2 == 0 else nc.scalar.copy
 
@@ -155,12 +185,13 @@ def tile_detect_w_kernel(tc, x0, x1, W0_words, W0_scales, b0, W1_words, W1_scale
                     nc.tensor.transpose(out=tp[:, P * t : P * (t + 1)], in_=t1f[:, 8 * t + sg : ROW // 2 : 32],
                                         identity=ident[:])
                 tv = tp[:].bitcast(BF16).rearrange("p (t q z e) -> p t q z e", t=4, z=2, e=2)
-                cells = slice(2 * sg, 2 * sg + 2)
-                copier(sg)(out=g5[:, 0:8, cells, :, :],
+                xs = slice(2 * (sg % 2), 2 * (sg % 2) + 2)
+                y = sg // 2
+                copier(sg)(out=g6[:, 0:8, xs, y, :, :],
                            in_=tv[:, :, :, 0, :].rearrange("p t (b g) e -> p g e b t", g=8))
-                copier(sg)(out=g5[:, 8:20, cells, 0:5, :],
+                copier(sg)(out=g6[:, 8:20, xs, y, 0:5, :],
                            in_=tv[:, :, 0:60, 1, :].rearrange("p t (b g) e -> p g e b t", g=12))
-                copier(sg)(out=g5[:, 8:12, cells, 5, :],
+                copier(sg)(out=g6[:, 8:12, xs, y, 5, :],
                            in_=tv[:, :, 60:64, 1, :].rearrange("p t g e -> p g e t"))
             quantise(0, 8)
 
@@ -170,10 +201,11 @@ def tile_detect_w_kernel(tc, x0, x1, W0_words, W0_scales, b0, W1_words, W1_scale
                     nc.tensor.transpose(out=tq[:, P * t : P * (t + 1)], in_=t2f[:, 8 * t + sg : ROW // 2 : 32],
                                         identity=ident[:])
                 tw = tq[:].bitcast(BF16).rearrange("p (t r z e) -> p t r z e", t=4, z=4, e=2)
-                cells = slice(2 * sg, 2 * sg + 2)
-                copier(sg)(out=g5[:, 12:20, cells, 5, :],
+                xs = slice(2 * (sg % 2), 2 * (sg % 2) + 2)
+                y = sg // 2
+                copier(sg)(out=g6[:, 12:20, xs, y, 5, :],
                            in_=tw[:, :, 0:8, 0, :].rearrange("p t g e -> p g e t"))
-                copier(sg)(out=g5[:, 8:20, cells, 6:8, :],
+                copier(sg)(out=g6[:, 8:20, xs, y, 6:8, :],
                            in_=tw[:, :, 8:32, 0, :].rearrange("p t (b g) e -> p g e b t", g=12))
 
             mx_group(0)
@@ -188,75 +220,84 @@ def tile_detect_w_kernel(tc, x0, x1, W0_words, W0_scales, b0, W1_words, W1_scale
             quantise(16, 20)
             mx_group(4)
             mx_group(5)
-            for lv in (0, 1):
-                for (c0, cn) in CHUNKS:
-                    bp = psum.tile([P, 512], F32, name="bp", tag="bank")
-                    nc.tensor.matmul(out=bp[:, :cn], lhsT=ones[:], rhs=brow[:, lv, c0 : c0 + cn], start=True, stop=True)
-                    nc.scalar.copy(out=bias_bc[:, lv, c0 : c0 + cn], in_=bp[:, :cn])
-                bb = bias_bc[:, lv, :].rearrange("p (i j f) -> p i j f", i=3, j=6)
-                for i in range(3):
-                    for d in range(2):
-                        nc.vector.tensor_scalar_add(out=bb[:, i, :, 2 + d : 3 + d], in0=bb[:, i, :, 2 + d : 3 + d],
-                                                    scalar1=math.log((ANCH[lv][i][d] / STRIDES[lv]) * STRIDES[lv]))
-                for j in range(6):
-                    nc.vector.tensor_scalar_add(out=bb[:, :, j, 4:5], in0=bb[:, :, j, 4:5],
-                                                scalar1=RAD * ANGLES_DEG[j])
+            bp = psum.tile([P, 512], F32, name="bp", tag="bank")
+            nc.tensor.transpose(out=bp[:, :P], in_=bf[:], identity=ident[:])
+            nc.vector.tensor_copy(out=bcol[:], in_=bp[:, 0:64])
 
-        resp = ctx.enter_context(tc.tile_pool(name="resp", bufs=10))
-        tmp = ctx.enter_context(tc.tile_pool(name="tmp", bufs=3))
+        resp = ctx.enter_context(tc.tile_pool(name="resp", bufs=6))
+        tmp = ctx.enter_context(tc.tile_pool(name="tmp", bufs=5))
         late = ctx.enter_context(tc.tile_pool(name="late", bufs=1))
         wtail = late.tile([P, 2, 4 * NO], U8, name="wtail", align_bytes=64)
 
-        def decode_a(lv, j, acc):
-            c0, cn = CHUNKS[j]
-            na = cn // NF
-            pre = tmp.tile([P, 512], F32, name="pre")
-            inv = tmp.tile([P, 4, 2], F32, name="inv")
+        def add_bias(lv, j, acc):
+            a0, na = CHUNKS[j]
+            z = tmp.tile([P, 512], F32, name="z")
+            if na == 4:
+                nc.vector.tensor_tensor(
+                    out=z[:].rearrange("p (x a r) -> p a x r", x=4, a=4),
+                    in0=acc[j][:].rearrange("p (a x r) -> p a x r", a=4, x=4),
+                    in1=bcol[:, 32 * lv + a0 : 32 * lv + a0 + 4].unsqueeze(2).unsqueeze(3).to_broadcast([P, 4, 4, 32]),
+                    op=ALU.add)
+            else:
+                for a in range(na):
+                    nc.vector.tensor_scalar(
+                        out=z[:, P * a : P * (a + 1)].rearrange("p (y x b) -> p x y b", y=4, x=4),
+                        in0=acc[j][:, P * a : P * (a + 1)].rearrange("p (x y b) -> p x y b", y=4, x=4),
+                        scalar1=bcol[:, 32 * lv + a0 + a : 32 * lv + a0 + a + 1], scalar2=None, op0=ALU.add)
+            return z
+
+        def turn(j, z):
+            na = CHUNKS[j][1]
+            tz = psum.tile([P, 512], F32, name="tz", tag="bank")
+            for x in range(na):
+                nc.tensor.transpose(out=tz[:, P * x : P * (x + 1)], in_=z[:, P * x : P * (x + 1)], identity=ident[:])
+            return tz
+
+        def decode(lv, j, tz, eng):
+            a0, na = CHUNKS[j]
+            cn = na * NF
             res = resp.tile([P, 512], F32, name="res")
-            pre3 = pre[:, :cn].rearrange("p (a f) -> p a f", f=NF)
-            nc.vector.tensor_tensor(out=pre[:, :cn], in0=acc[j][:, :cn], in1=bias_bc[:, lv, c0 : c0 + cn], op=ALU.add)
-            nc.scalar.activation(out=inv[:, :na, :], in_=pre3[:, :, 2:4], func=ACT.Sigmoid, scale=-1.0)
-            nc.scalar.activation(out=res[:, :cn], in_=pre[:, :cn], func=ACT.Sigmoid)
-            return (lv, j, pre, inv, res)
-
-        def decode_b(state, eng):
-            lv, j, pre, inv, res = state
-            c0, cn = CHUNKS[j]
-            a0 = c0 // NF
-            na = cn // NF
-            pre3 = pre[:, :cn].rearrange("p (a f) -> p a f", f=NF)
-            res3 = res[:, :cn].rearrange("p (a f) -> p a f", f=NF)
+            inv = tmp.tile([P, 4, 2], F32, name="inv")
+            tz3 = tz[:, :cn].rearrange("p (x f) -> p x f", f=NF)
+            res3 = res[:, :cn].rearrange("p (x f) -> p x f", f=NF)
+            nc.scalar.activation(out=inv[:, :na, :], in_=tz3[:, :, 2:4], func=ACT.Sigmoid, scale=-1.0)
+            nc.scalar.activation(out=res3[:, :, 0:4], in_=tz3[:, :, 0:4], func=ACT.Sigmoid)
+            nc.scalar.copy(out=res3[:, :, 4:5], in_=tz3[:, :, 4:5])
+            nc.scalar.activation(out=res3[:, :, 5:NF], in_=tz3[:, :, 5:NF], func=ACT.Sigmoid)
+            grid = grid4[:, lv, :, :] if na == 4 else grid1[:, lv, :].unsqueeze(1).to_broadcast([P, na, 2])
             nc.vector.reciprocal(out=inv[:, :na, :], in_=inv[:, :na, :])
+            nc.vector.scalar_tensor_tensor(out=res3[:, :, 0:2], in0=res3[:, :, 0:2], scalar=SXY[lv] * STRIDES[lv], in1=grid,
+                                           op0=ALU.mult, op1=ALU.add)
             nc.vector.tensor_tensor(out=res3[:, :, 2:4], in0=res3[:, :, 2:4], in1=inv[:, :na, :], op=ALU.mult)
-            nc.vector.scalar_tensor_tensor(
-                out=res3[:, :, 0:2], in0=res3[:, :, 0:2], scalar=SXY[lv] * STRIDES[lv],
-                in1=gxy[:, lv, :].unsqueeze(1).to_broadcast([P, na, 2]), op0=ALU.mult, op1=ALU.add)
-            nc.vector.tensor_copy(out=res3[:, :, 4:5], in_=pre3[:, :, 4:5])
-            for a in range(na):
-                r0 = 288 * lv + CELLS * (a0 + a)
-                eng.dma_start(out=out[:, r0 : r0 + CELLS, :].rearrange("b s f -> s b f"), in_=res3[:, a, :])
+            r0 = 288 * lv + 16 * a0
+            if na == 4:
+                eng.dma_start(out=out[:, r0 : r0 + 64, :].rearrange("b (q x) f -> q b (x f)", x=4), in_=res[:])
+            else:
+                for a in range(na):
+                    eng.dma_start(out=out[:, r0 + 16 * a : r0 + 16 * (a + 1), :].rearrange("b s f -> s b f"), in_=res3[:, a, :])
 
-        for (c0, cn) in CHUNKS:
+        for (a0, na) in CHUNKS:
+            c0, c1 = P * a0, P * (a0 + na)
             nc.sync.dma_start(
-                out=wtail[:, :, 4 * c0 : 4 * (c0 + cn)].bitcast(I32),
-                in_=words[1][TAIL_G[0] : TAIL_G[1] + 1, :, c0 : c0 + cn, :].rearrange("g p n t -> p g (n t)").bitcast(I32))
+                out=wtail[:, :, 4 * c0 : 4 * c1].bitcast(I32),
+                in_=words[1][TAIL_G[0] : TAIL_G[1] + 1, :, c0:c1, :].rearrange("g p n t -> p g (n t)").bitcast(I32))
         mx_group(6)
         mx_group(7)
-        prev = None
-        for j in range(len(CHUNKS)):
-            cur = decode_a(0, j, accs[0])
-            if prev is not None:
-                decode_b(prev, nc.gpsimd)
-            prev = cur
-        decode_b(prev, nc.gpsimd)
-        for i in range(8, len(seq)):
+        zs = [add_bias(0, j, accs[0]) for j in range(len(CHUNKS))]
+        mx_group(8)
+        for j in range(3):
+            decode(0, j, turn(j, zs[j]), nc.gpsimd)
+        mx_group(9)
+        for j in range(3, 5):
+            decode(0, j, turn(j, zs[j]), nc.gpsimd)
+        for i in range(10, len(seq)):
             mx_group(i)
         prev = None
-        for j, (c0, cn) in enumerate(CHUNKS):
+        for j, (a0, na) in enumerate(CHUNKS):
             for u in range(2):
-                passes(accs[1], j, GOFF[1] + TAIL_G[u], wtail[:, u, 4 * c0 : 4 * (c0 + cn)], False, u == 1)
-            cur = decode_a(1, j, accs[1])
+                passes(accs[1], j, GOFF[1] + TAIL_G[u], wtail[:, u, 4 * P * a0 : 4 * P * (a0 + na)], False, u == 1)
+            z = add_bias(1, j, accs[1])
             if prev is not None:
-                decode_b(prev, nc.sync)
-            prev = cur
-        decode_b(prev, nc.sync)
+                decode(1, j - 1, turn(j - 1, prev), nc.sync)
+            prev = z
+        decode(1, 4, turn(4, prev), nc.sync)

@@ -49,6 +49,7 @@ def tile_detect_w_kernel(tc, x0, x1, W0_words, W0_scales, b0, W1_words, W1_scale
         xplanes = keep.tile([P, NGROUPS, P], U8, name="xplanes", align_bytes=64)
         ident = keep.tile([P, P], F32, name="ident")
         bcol = keep.tile([P, 64], F32, name="bcol")
+        step = keep.tile([P, NGROUPS // 4, 16], F32, name="step")
         pint = keep.tile([P, 1], I32, name="pint")
         xint = keep.tile([P, 4], I32, name="xint")
         gint = keep.tile([P, 3], I32, name="gint")
@@ -70,11 +71,10 @@ def tile_detect_w_kernel(tc, x0, x1, W0_words, W0_scales, b0, W1_words, W1_scale
         def load_planes(j):
             lv = 0 if j < 2 else 1
             jj = j - GOFF[lv] // 4
-            for q in range(4):
-                nc.gpsimd.dma_start(
-                    out=planes[32 * q : 32 * q + 16, j, :].bitcast(F32),
-                    in_=scl[lv][4 * jj : 4 * jj + 4, 4 * q : 4 * q + 4, :].bitcast(F32),
-                )
+            for q in (0, 2, 1, 3):
+                rows = scl[lv][4 * jj : 4 * jj + 4, 4 * q : 4 * q + 4, :].bitcast(F32)
+                nc.gpsimd.dma_start(out=planes[32 * q : 32 * q + 16, j, :].bitcast(F32), in_=rows)
+                nc.gpsimd.dma_start(out=step[32 * q + 16 : 32 * q + 32, j, :], in_=rows[:, :, 0:16])
 
         def passes(acc, j, gg, wcols, first, last):
             a0, na = CHUNKS[j]

@@ -224,7 +224,7 @@ def tile_detect_w_kernel(tc, x0, x1, W0_words, W0_scales, b0, W1_words, W1_scale
             nc.tensor.transpose(out=bp[:, :P], in_=bf[:], identity=ident[:])
             nc.vector.tensor_copy(out=bcol[:], in_=bp[:, 0:64])
 
-        resp = ctx.enter_context(tc.tile_pool(name="resp", bufs=6))
+        resp = ctx.enter_context(tc.tile_pool(name="resp", bufs=10))
         tmp = ctx.enter_context(tc.tile_pool(name="tmp", bufs=5))
         late = ctx.enter_context(tc.tile_pool(name="late", bufs=1))
         wtail = late.tile([P, 2, 4 * NO], U8, name="wtail", align_bytes=64)
@@ -286,10 +286,10 @@ def tile_detect_w_kernel(tc, x0, x1, W0_words, W0_scales, b0, W1_words, W1_scale
         zs = [add_bias(0, j, accs[0]) for j in range(len(CHUNKS))]
         mx_group(8)
         for j in range(3):
-            decode(0, j, turn(j, zs[j]), nc.gpsimd)
+            decode(0, j, turn(j, zs[j]), nc.sync)
         mx_group(9)
         for j in range(3, 5):
-            decode(0, j, turn(j, zs[j]), nc.gpsimd)
+            decode(0, j, turn(j, zs[j]), nc.sync)
         for i in range(10, len(seq)):
             mx_group(i)
         prev = None

@@ -68,13 +68,19 @@ def tile_detect_w_kernel(tc, x0, x1, W0_words, W0_scales, b0, W1_words, W1_scale
                               in_=words[lv][g].rearrange("p n t -> p (n t)").bitcast(I32))
             wts.append(wt)
 
-        def load_planes(j):
+        def load_planes(j, t2, x1v):
             lv = 0 if j < 2 else 1
             jj = j - GOFF[lv] // 4
-            for q in (0, 2, 1, 3):
+            for k, q in enumerate((0, 2, 1, 3)):
                 rows = scl[lv][4 * jj : 4 * jj + 4, 4 * q : 4 * q + 4, :].bitcast(F32)
                 nc.gpsimd.dma_start(out=planes[32 * q : 32 * q + 16, j, :].bitcast(F32), in_=rows)
-                nc.gpsimd.dma_start(out=step[32 * q + 16 : 32 * q + 32, j, :], in_=rows[:, :, 0:16])
+                if j == 1:
+                    base = 32 * q + 16
+                    r0 = 64 + 8 * k
+                    nc.gpsimd.dma_start(out=t2[base : base + 15 : 2, :],
+                                        in_=x1v[r0 : r0 + 8, :].rearrange("(m c) f -> c m f", m=2))
+                else:
+                    nc.gpsimd.dma_start(out=step[32 * q + 16 : 32 * q + 32, j, :], in_=rows[:, :, 0:16])
 
         def passes(acc, j, gg, wcols, first, last):
             a0, na = CHUNKS[j]
@@ -121,16 +127,13 @@ def tile_detect_w_kernel(tc, x0, x1, W0_words, W0_scales, b0, W1_words, W1_scale
             nc.sync.dma_start(out=t1[1:128:2, :], in_=x1v[0:64])
             for lv in range(2):
                 nc.scalar.dma_start(out=brow[32 * lv : 32 * lv + NA, :], in_=bs[lv].rearrange("(a f) -> a f", f=NF))
-            for i in range(2):
-                load_w(i)
-            nc.sync.dma_start(out=t2[0:128:4, :], in_=x1v[64:96])
-            for i in range(2, W_BUFS):
+            for i in range(W_BUFS):
                 load_w(i)
 
             nc.gpsimd.iota(out=pint[:], pattern=[[0, 1]], base=0, channel_multiplier=1)
             nc.gpsimd.iota(out=xint[:], pattern=[[1, 4]], base=0, channel_multiplier=0)
             for j in range(NGROUPS // 4):
-                load_planes(j)
+                load_planes(j, t2, x1v)
 
             nc.vector.tensor_scalar(out=gint[:, 0:1], in0=pint[:], scalar1=3, scalar2=3,
                                     op0=ALU.logical_shift_right, op1=ALU.bitwise_and)
@@ -200,13 +203,13 @@ def tile_detect_w_kernel(tc, x0, x1, W0_words, W0_scales, b0, W1_words, W1_scale
                 for t in range(4):
                     nc.tensor.transpose(out=tq[:, P * t : P * (t + 1)], in_=t2f[:, 8 * t + sg : ROW // 2 : 32],
                                         identity=ident[:])
-                tw = tq[:].bitcast(BF16).rearrange("p (t r z e) -> p t r z e", t=4, z=4, e=2)
+                tw = tq[:].bitcast(BF16).rearrange("p (t u r e) -> p t u r e", t=4, u=8, e=2)
                 xs = slice(2 * (sg % 2), 2 * (sg % 2) + 2)
                 y = sg // 2
-                copier(sg)(out=g6[:, 12:20, xs, y, 5, :],
-                           in_=tw[:, :, 0:8, 0, :].rearrange("p t g e -> p g e t"))
-                copier(sg)(out=g6[:, 8:20, xs, y, 6:8, :],
-                           in_=tw[:, :, 8:32, 0, :].rearrange("p t (b g) e -> p g e b t", g=12))
+                for (u, m0, m1, b, g0) in ((1, 0, 2, 5, 4), (5, 0, 2, 6, 0), (3, 0, 1, 6, 8), (3, 1, 2, 7, 0), (7, 0, 2, 7, 4)):
+                    rows = tw[:, :, u, :, :].rearrange("p t (c m z) e -> p t c m z e", c=4, m=2)[:, :, :, m0:m1, 0, :]
+                    copier(sg)(out=g6[:, 8 + g0 : 8 + g0 + 4 * (m1 - m0), xs, y, b, :].rearrange("p (m c) e t -> p m c e t", c=4),
+                               in_=rows.rearrange("p t c m e -> p m c e t"))
 
             mx_group(0)
             mx_group(1)

import math
from contextlib import ExitStack

import concourse.mybir as mybir
from concourse.masks import make_identity

F32 = mybir.dt.float32
BF16 = mybir.dt.bfloat16
I32 = mybir.dt.int32
U8 = mybir.dt.uint8
U32 = mybir.dt.uint32
FP8X4 = mybir.dt.float8_e4m3fn_x4
ALU = mybir.AluOpType
ACT = mybir.ActivationFunctionType

P = 128
BATCH = 8
NA = 18
NF = 128
NO = NA * NF
GROUPS = [8, 12]
GOFF = [0, 8]
NGROUPS = 20
ROW = 8192
STRIDES = [8.0, 16.0]
SXY = [1.2, 1.1]
ANCH = [[[10, 13], [16, 30], [33, 23]], [[30, 61], [62, 45], [59, 119]]]
RAD = 3.141592653589793 / 180.0
CHUNKS = [(0, 4), (4, 4), (8, 4), (12, 4), (16, 2)]
W_BUFS = 12
TAIL_G = [10, 11]

FLOPS = 2 * 128 * (4096 + 6144) * NO


def tile_detect_w_kernel(tc, x0, x1, W0_words, W0_scales, b0, W1_words, W1_scales, b1, out):
    nc = tc.nc
    words = [W0_words, W1_words]
    scl = [W0_scales, W1_scales]
    bs = [b0, b1]
    with ExitStack() as ctx:
        ctx.enter_context(tc.manual_schedule())
        keep = ctx.enter_context(tc.tile_pool(name="keep", bufs=1))
        wpool = ctx.enter_context(tc.tile_pool(name="wpool", bufs=W_BUFS))
        psum = ctx.enter_context(tc.psum_pool(name="psum", bufs=8))

        planes = keep.tile([P, NGROUPS // 4, NO], U8, name="planes", align_bytes=64)
        xcodes = keep.tile([P, NGROUPS, P], U32, name="xcodes", align_bytes=64)
        xplanes = keep.tile([P, NGROUPS, P], U8, name="xplanes", align_bytes=64)
        ident = keep.tile([P, P], F32, name="ident")
        bcol = keep.tile([P, 64], F32, name="bcol")
        step = keep.tile([P, NGROUPS // 4, 16], F32, name="step")
        pint = keep.tile([P, 1], I32, name="pint")
        xint = keep.tile([P, 4], I32, name="xint")
        gint = keep.tile([P, 3], I32, name="gint")
        gflt = keep.tile([P, 3], F32, name="gflt")
        xflt = keep.tile([P, 4], F32, name="xflt")
        ge = keep.tile([P, 2], F32, name="ge")
        grid4 = keep.tile([P, 2, 4, 2], F32, name="grid4")
        grid1 = keep.tile([P, 2, 2], F32, name="grid1")
        wts = []
        seq = [(0, g) for g in range(8)] + [(1, g) for g in range(10)]

        def load_w(i):
            lv, g = seq[i]
            wt = wpool.tile([P, 4 * NO], U8, name="wt", align_bytes=64)
            nc.sync.dma_start(out=wt[:].bitcast(I32),
                              in_=words[lv][g].rearrange("p n t -> p (n t)").bitcast(I32))
            wts.append(wt)

        def load_planes(j, t2, x1v):
            lv = 0 if j < 2 else 1
            jj = j - GOFF[lv] // 4
            for k, q in enumerate((0, 2, 1, 3)):
                rows = scl[lv][4 * jj : 4 * jj + 4, 4 * q : 4 * q + 4, :].bitcast(F32)
                nc.gpsimd.dma_start(out=planes[32 * q : 32 * q + 16, j, :].bitcast(F32), in_=rows)
                if j == 1:
                    base = 32 * q + 16
                    r0 = 64 + 8 * k
                    nc.gpsimd.dma_start(out=t2[base : base + 15 : 2, :],
                                        in_=x1v[r0 : r0 + 8, :].rearrange("(m c) f -> c m f", m=2))
                else:
                    nc.gpsimd.dma_start(out=step[32 * q + 16 : 32 * q + 32, j, :], in_=rows[:, :, 0:16])

        def passes(acc, j, gg, wcols, first, last):
            a0, na = CHUNKS[j]
            k0 = 4 * (gg % 4)
            for a in range(na):
                c = P * (a0 + a)
                nc.tensor.matmul_mx(
                    out=acc[j][:, P * a : P * (a + 1)],
                    lhsT=wcols[:, 4 * P * a : 4 * P * (a + 1)].bitcast(FP8X4),
                    lhsT_scale=planes[k0:P, gg // 4, c : c + P],
                    rhs=xcodes[:, gg, :].bitcast(FP8X4),
                    rhs_scale=xplanes[:, gg, :],
                    start=first and a == 0,
                    stop=last and a == na - 1,
                )

        accs = [None, None]

        def mx_group(i):
            lv, g = seq[i]
            if g == 0:
                accs[lv] = [psum.tile([P, 512], F32, name="acc%d_%d" % (lv, j), tag="bank") for j in range(len(CHUNKS))]
            for j, (a0, na) in enumerate(CHUNKS):
                passes(accs[lv], j, GOFF[lv] + g, wts[i][:, 4 * P * a0 : 4 * P * (a0 + na)], g == 0,
                       lv == 0 and g == GROUPS[0] - 1)
            if i + W_BUFS < len(seq):
                load_w(i + W_BUFS)

        with tc.tile_pool(name="prep", bufs=1) as prep:
            t1 = prep.tile([P, ROW], BF16, name="t1")
            t2 = prep.tile([P, ROW], BF16, name="t2")
            grouped = prep.tile([P, NGROUPS, 4 * P], BF16, name="grouped", align_bytes=64)
            brow = prep.tile([P, NF], BF16, name="brow")
            bf = prep.tile([P, NF], F32, name="bf")

            nc.vector.memset(brow[:], 0.0)
            nc.vector.memset(planes[:].bitcast(I32), 0)
            nc.vector.memset(t2[:].bitcast(I32), 0)
            make_identity(nc, ident[:])

            x0v = x0.rearrange("b (g r) h w -> (b g) (r h w)", g=GROUPS[0])
            x1v = x1.rearrange("b (g r) h w -> (b g) (r h w)", g=GROUPS[1])
            nc.sync.dma_start(out=t1[0:128:2, :], in_=x0v)
            nc.sync.dma_start(out=t1[1:128:2, :], in_=x1v[0:64])
            for lv in range(2):
                nc.scalar.dma_start(out=brow[32 * lv : 32 * lv + NA, :], in_=bs[lv].rearrange("(a f) -> a f", f=NF))
            for i in range(W_BUFS):
                load_w(i)

            nc.gpsimd.iota(out=pint[:], pattern=[[0, 1]], base=0, channel_multiplier=1)
            nc.gpsimd.iota(out=xint[:], pattern=[[1, 4]], base=0, channel_multiplier=0)
            for j in range(NGROUPS // 4):
                load_planes(j, t2, x1v)

            nc.vector.tensor_scalar(out=gint[:, 0:1], in0=pint[:], scalar1=3, scalar2=3,
                                    op0=ALU.logical_shift_right, op1=ALU.bitwise_and)
            nc.vector.tensor_scalar(out=gint[:, 1:2], in0=pint[:], scalar1=5, scalar2=3,
                                    op0=ALU.logical_shift_right, op1=ALU.bitwise_and)
            nc.vector.tensor_scalar(out=gint[:, 2:3], in0=pint[:], scalar1=31, scalar2=None, op0=ALU.bitwise_and)
            nc.vector.tensor_copy(out=gflt[:], in_=gint[:])
            nc.vector.tensor_copy(out=xflt[:], in_=xint[:])
            for lv in range(2):
                s = STRIDES[lv]
                off = -s * (SXY[lv] - 1.0) / 2.0
                nc.vector.tensor_scalar(out=grid4[:, lv, :, 0], in0=xflt[:], scalar1=s, scalar2=off, op0=ALU.mult, op1=ALU.add)
                nc.vector.tensor_scalar(out=grid4[:, lv, :, 1], in0=gflt[:, 0:1].to_broadcast([P, 4]), scalar1=s, scalar2=off,
                                        op0=ALU.mult, op1=ALU.add)
                nc.vector.tensor_scalar(out=grid1[:, lv, :], in0=gflt[:, 0:2], scalar1=s, scalar2=off, op0=ALU.mult, op1=ALU.add)
            nc.vector.tensor_copy(out=bf[:], in_=brow[:])
            nc.vector.tensor_scalar(out=ge[:, 0:1], in0=gflt[:, 2:3], scalar1=5.5, scalar2=None, op0=ALU.is_ge)
            nc.vector.tensor_scalar(out=ge[:, 1:2], in0=gflt[:, 2:3], scalar1=11.5, scalar2=None, op0=ALU.is_ge)
            for lv in range(2):
                rows = slice(32 * lv, 32 * lv + 32)
                for d in range(2):
                    sizes = [math.log((ANCH[lv][i][d] / STRIDES[lv]) * STRIDES[lv]) for i in range(3)]
                    col = bf[rows, 2 + d : 3 + d]
                    nc.vector.tensor_scalar_add(out=col, in0=col, scalar1=sizes[0])
                    for i in range(2):
                        nc.vector.scalar_tensor_tensor(out=col, in0=ge[rows, i : i + 1], scalar=sizes[i + 1] - sizes[i],
                                                       in1=col, op0=ALU.mult, op1=ALU.add)
            col = bf[:, 4:5]
            nc.vector.tensor_scalar_add(out=col, in0=col, scalar1=-60.0 * RAD)
            nc.vector.scalar_tensor_tensor(out=col, in0=gflt[:, 2:3], scalar=30.0 * RAD, in1=col, op0=ALU.mult, op1=ALU.add)
            for i in range(2):
                nc.vector.scalar_tensor_tensor(out=col, in0=ge[:, i : i + 1], scalar=-180.0 * RAD, in1=col,
                                               op0=ALU.mult, op1=ALU.add)

            g6 = grouped[:].rearrange("p g (x y b t) -> p g x y b t", x=4, y=4, b=BATCH)
            t1f = t1[:].bitcast(F32)
            t2f = t2[:].bitcast(F32)

            def copier(sg):
                return nc.vector.tensor_copy if sg % 2 == 0 else nc.scalar.copy

            def quantise(g0, g1):
                nc.vector.quantize_mx(
                    out=xcodes[:, g0:g1, :].rearrange("p g m -> p (g m)").bitcast(FP8X4),
                    scales=xplanes[:, g0:g1, :].rearrange("p g m -> p (g m)"),
                    in_=grouped[:, g0:g1, :].rearrange("p g c -> p (g c)"),
                )

            for sg in range(8):
                tp = psum.tile([P, 512], F32, name="tp", tag="bank")
                for t in range(4):
                    nc.tensor.transpose(out=tp[:, P * t : P * (t + 1)], in_=t1f[:, 8 * t + sg : ROW // 2 : 32],
                                        identity=ident[:])
                tv = tp[:].bitcast(BF16).rearrange("p (t q z e) -> p t q z e", t=4, z=2, e=2)
                xs = slice(2 * (sg % 2), 2 * (sg % 2) + 2)
                y = sg // 2
                copier(sg)(out=g6[:, 0:8, xs, y, :, :],
                           in_=tv[:, :, :, 0, :].rearrange("p t (b g) e -> p g e b t", g=8))
                copier(sg)(out=g6[:, 8:20, xs, y, 0:5, :],
                           in_=tv[:, :, 0:60, 1, :].rearrange("p t (b g) e -> p g e b t", g=12))
                copier(sg)(out=g6[:, 8:12, xs, y, 5, :],
                           in_=tv[:, :, 60:64, 1, :].rearrange("p t g e -> p g e t"))
            quantise(0, 8)

            def second_tile(sg):
                tq = psum.tile([P, 512], F32, name="tq", tag="bank")
                for t in range(4):
                    nc.tensor.transpose(out=tq[:, P * t : P * (t + 1)], in_=t2f[:, 8 * t + sg : ROW // 2 : 32],
                                        identity=ident[:])
                tw = tq[:].bitcast(BF16).rearrange("p (t u r e) -> p t u r e", t=4, u=8, e=2)
                xs = slice(2 * (sg % 2), 2 * (sg % 2) + 2)
                y = sg // 2
                for (u, m0, m1, b, g0) in ((1, 0, 2, 5, 4), (5, 0, 2, 6, 0), (3, 0, 1, 6, 8), (3, 1, 2, 7, 0), (7, 0, 2, 7, 4)):
                    rows = tw[:, :, u, :, :].rearrange("p t (c m z) e -> p t c m z e", c=4, m=2)[:, :, :, m0:m1, 0, :]
                    copier(sg)(out=g6[:, 8 + g0 : 8 + g0 + 4 * (m1 - m0), xs, y, b, :].rearrange("p (m c) e t -> p m c e t", c=4),
                               in_=rows.rearrange("p t c m e -> p m c e t"))

            mx_group(0)
            mx_group(1)
            for sg in range(0, 4):
                second_tile(sg)
            mx_group(2)
            mx_group(3)
            for sg in range(4, 8):
                second_tile(sg)
            quantise(8, 16)
            quantise(16, 20)
            mx_group(4)
            mx_group(5)
            bp = psum.tile([P, 512], F32, name="bp", tag="bank")
            nc.tensor.transpose(out=bp[:, :P], in_=bf[:], identity=ident[:])
            nc.vector.tensor_copy(out=bcol[:], in_=bp[:, 0:64])

        resp = ctx.enter_context(tc.tile_pool(name="resp", bufs=10))
        tmp = ctx.enter_context(tc.tile_pool(name="tmp", bufs=5))
        late = ctx.enter_context(tc.tile_pool(name="late", bufs=1))
        wtail = late.tile([P, 2, 4 * NO], U8, name="wtail", align_bytes=64)

        def add_bias(lv, j, acc):
            a0, na = CHUNKS[j]
            z = tmp.tile([P, 512], F32, name="z")
            if na == 4:
                nc.vector.tensor_tensor(
                    out=z[:].rearrange("p (x a r) -> p a x r", x=4, a=4),
                    in0=acc[j][:].rearrange("p (a x r) -> p a x r", a=4, x=4),
                    in1=bcol[:, 32 * lv + a0 : 32 * lv + a0 + 4].unsqueeze(2).unsqueeze(3).to_broadcast([P, 4, 4, 32]),
                    op=ALU.add)
            else:
                for a in range(na):
                    nc.vector.tensor_scalar(
                        out=z[:, P * a : P * (a + 1)].rearrange("p (y x b) -> p x y b", y=4, x=4),
                        in0=acc[j][:, P * a : P * (a + 1)].rearrange("p (x y b) -> p x y b", y=4, x=4),
                        scalar1=bcol[:, 32 * lv + a0 + a : 32 * lv + a0 + a + 1], scalar2=None, op0=ALU.add)
            return z

        def turn(j, z):
            na = CHUNKS[j][1]
            tz = psum.tile([P, 512], F32, name="tz", tag="bank")
            for x in range(na):
                nc.tensor.transpose(out=tz[:, P * x : P * (x + 1)], in_=z[:, P * x : P * (x + 1)], identity=ident[:])
            return tz

        def decode(lv, j, tz, eng):
            a0, na = CHUNKS[j]
            cn = na * NF
            res = resp.tile([P, 512], F32, name="res")
            inv = tmp.tile([P, 4, 2], F32, name="inv")
            tz3 = tz[:, :cn].rearrange("p (x f) -> p x f", f=NF)
            res3 = res[:, :cn].rearrange("p (x f) -> p x f", f=NF)
            nc.scalar.activation(out=inv[:, :na, :], in_=tz3[:, :, 2:4], func=ACT.Sigmoid, scale=-1.0)
            nc.scalar.activation(out=res3[:, :, 0:4], in_=tz3[:, :, 0:4], func=ACT.Sigmoid)
            nc.scalar.copy(out=res3[:, :, 4:5], in_=tz3[:, :, 4:5])
            nc.scalar.activation(out=res3[:, :, 5:NF], in_=tz3[:, :, 5:NF], func=ACT.Sigmoid)
            grid = grid4[:, lv, :, :] if na == 4 else grid1[:, lv, :].unsqueeze(1).to_broadcast([P, na, 2])
            nc.vector.reciprocal(out=inv[:, :na, :], in_=inv[:, :na, :])
            nc.vector.scalar_tensor_tensor(out=res3[:, :, 0:2], in0=res3[:, :, 0:2], scalar=SXY[lv] * STRIDES[lv], in1=grid,
                                           op0=ALU.mult, op1=ALU.add)
            nc.vector.tensor_tensor(out=res3[:, :, 2:4], in0=res3[:, :, 2:4], in1=inv[:, :na, :], op=ALU.mult)
            r0 = 288 * lv + 16 * a0
            if na == 4:
                eng.dma_start(out=out[:, r0 : r0 + 64, :].rearrange("b (q x) f -> q b (x f)", x=4), in_=res[:])
            else:
                for a in range(na):
                    eng.dma_start(out=out[:, r0 + 16 * a : r0 + 16 * (a + 1), :].rearrange("b s f -> s b f"), in_=res3[:, a, :])

        for (a0, na) in CHUNKS:
            c0, c1 = P * a0, P * (a0 + na)
            nc.sync.dma_start(
                out=wtail[:, :, 4 * c0 : 4 * c1].bitcast(I32),
                in_=words[1][TAIL_G[0] : TAIL_G[1] + 1, :, c0:c1, :].rearrange("g p n t -> p g (n t)").bitcast(I32))
        mx_group(6)
        mx_group(7)
        zs = [add_bias(0, j, accs[0]) for j in range(len(CHUNKS))]
        mx_group(8)
        for j in range(3):
            decode(0, j, turn(j, zs[j]), nc.sync)
        mx_group(9)
        for j in range(3, 5):
            decode(0, j, turn(j, zs[j]), nc.sync)
        for i in range(10, len(seq)):
            mx_group(i)
        prev = None
        for j, (a0, na) in enumerate(CHUNKS):
            for u in range(2):
                passes(accs[1], j, GOFF[1] + TAIL_G[u], wtail[:, u, 4 * P * a0 : 4 * P * (a0 + na)], False, u == 1)
            z = add_bias(1, j, accs[1])
            if prev is not None:
                decode(1, j - 1, turn(j - 1, prev), nc.sync)
            prev = z
        decode(1, 4, turn(4, prev), nc.sync)
